import numpy as np
import ml_dtypes


def mxq(x, axis, fmt="e4m3"):
    dtype, down = {"e4m3": (ml_dtypes.float8_e4m3fn, 7), "e5m2": (ml_dtypes.float8_e5m2, 14)}[fmt]
    v = np.moveaxis(np.asarray(x, np.float32).astype(ml_dtypes.bfloat16).astype(np.float64), axis, -1)
    blocks = v.reshape(v.shape[:-1] + (-1, 32))
    amax = np.abs(blocks).max(-1, keepdims=True)
    byte = np.maximum(np.where(amax > 0, np.frexp(amax)[1] - 1 + 127, 0) - down, 1)
    scale = np.exp2(byte - 127.0)
    codes = (blocks / scale).astype(np.float32).astype(dtype).astype(np.float64)
    return np.moveaxis((codes * scale).reshape(v.shape), -1, axis)


WIDE = False


def mx_kscale(k):
    if not WIDE:
        return np.ones(k)
    levels = np.array([10, -10, 5, -5, 0])
    if k % 512:
        return np.exp2(np.random.permutation(np.resize(levels, k // 32))).repeat(32)
    a = np.empty((k // 512, 16))
    for p in range(k // 512):
        a[p, :8] = np.random.permutation(np.resize(levels, 8))
        for g in range(8):
            far = levels[np.abs(levels - a[p, g]) >= 10]
            a[p, g + 8] = far[np.random.randint(len(far))]
    return np.exp2(a.ravel()).repeat(32)


BF16 = ml_dtypes.bfloat16


def bf(x):
    return np.asarray(x, np.float32).astype(BF16)


def f64(x):
    return np.asarray(x).astype(np.float64)


B, N, C, DIM, H = 4, 1024, 512, 1024, 8
D = DIM // H // 2
LAYER_NUM = 12
LAM_INIT = 0.8 - 0.6 * np.exp(-0.3 * LAYER_NUM)
SCALE = D ** -0.5


def split_qk(y):
    y = y.reshape(B, N, H, D, 2)
    return np.moveaxis(y, -1, 2).reshape(B, N, 2 * H, D)


def setup_inputs():
    s = mx_kscale(C)
    ls = 0.45 / D ** 0.25
    return {"x": bf(np.random.standard_normal((B, N, C)) * s),
            "Wq": bf(np.random.standard_normal((DIM, C)) / np.sqrt(C) / s),
            "Wk": bf(np.random.standard_normal((DIM, C)) / np.sqrt(C) / s),
            "lq1": bf(np.random.standard_normal(D) * ls),
            "lq2": bf(np.random.standard_normal(D) * ls),
            "lk1": bf(np.random.standard_normal(D) * ls),
            "lk2": bf(np.random.standard_normal(D) * ls)}


def reference(x, Wq, Wk, lq1, lq2, lk1, lk2):
    xq = mxq(f64(x), 2, "e4m3")
    q = split_qk(xq @ mxq(f64(Wq), 1, "e4m3").T) * SCALE
    k = split_qk(xq @ mxq(f64(Wk), 1, "e4m3").T)
    sc = np.stack([(q[:, :, i:i + 1, :] * k).sum(-1) for i in range(2 * H)], axis=2)
    e = np.exp(sc - sc.max(-1, keepdims=True))
    att = e / e.sum(-1, keepdims=True)
    lam = np.exp(np.sum(f64(lq1) * f64(lk1))) - np.exp(np.sum(f64(lq2) * f64(lk2))) + LAM_INIT
    return att[:, :, :H, :H] - lam * att[:, :, H:, H:]

@@ -1,0 +1,392 @@
+import math
+
+import concourse.mybir as mybir
+from concourse.masks import make_identity
+
+F32 = mybir.dt.float32
+BF16 = mybir.dt.bfloat16
+I32 = mybir.dt.int32
+U32 = mybir.dt.uint32
+U8 = mybir.dt.uint8
+FP8X4 = mybir.dt.float8_e4m3fn_x4
+ALU = mybir.AluOpType
+ACT = mybir.ActivationFunctionType
+AXIS_X = mybir.AxisListType.X
+
+P = 128
+HALF = P // 2
+QUADRANT = 32
+TOKENS = 4 * 1024
+C = 512
+WORDS = C // 2
+ROWS = 16
+D = 64
+HEADS = 8
+BANK = 512
+BANK_ROWS = 4
+SCALE = D ** -0.5
+LAM_INIT = 0.8 - 0.6 * math.exp(-0.3 * 12)
+
+GROUP_TILES = 8
+GROUP_TOKENS = GROUP_TILES * P
+GROUPS = TOKENS // GROUP_TOKENS
+TENSOR_GROUPS = 3
+TILE_PAIRS = GROUP_TILES // 2
+BLOCKS = 4
+BLOCK_T = P // BLOCKS
+BLOCK_TOKENS = GROUP_TILES * BLOCK_T
+SCORE_COLS = ROWS * TILE_PAIRS
+BANK_MATMULS = BANK // SCORE_COLS
+
+PADDED = 2 * ROWS * D
+PADDED_ALL = PADDED + D
+
+CHUNK_ROWS = 2
+VECTOR_ROWS = BANK_ROWS
+BATCH_TILES = 4
+
+FLOPS = 2 * TOKENS * C * 2 * ROWS * D + 2 * TOKENS * ROWS * ROWS * D
+
+
+def transpose_words(nc, psum, ident, rows_f32, blocks):
+    planes = psum.tile([P, 2, blocks * P], F32, tag="planes")
+    for b in range(blocks):
+        for u in range(2):
+            nc.tensor.transpose(
+                planes[:, u, b * P : (b + 1) * P],
+                rows_f32[:, b * WORDS + u : (b + 1) * WORDS : 2],
+                ident[:],
+            )
+    return planes
+
+
+def tile_differentialattention_pa_t_kernel(tc, x, Wq, Wk, lq1, lq2, lk1, lk2, out):
+    nc = tc.nc
+    x_rows = x.flatten_outer_dims()
+    out_rows = out.rearrange("b n a h -> (b n) (a h)")
+
+    with (
+        tc.tile_pool(name="keep", bufs=1) as keep,
+        tc.tile_pool(name="stage", bufs=2) as stage,
+        tc.tile_pool(name="tensor_way", bufs=1) as tensor_way,
+        tc.tile_pool(name="vector_way", bufs=2) as vector_way,
+        tc.tile_pool(name="products", bufs=4) as products,
+        tc.psum_pool(name="psum_t", bufs=2) as psum_t,
+        tc.psum_pool(name="psum_y", bufs=3) as psum_y,
+        tc.psum_pool(name="psum_s", bufs=2) as psum_s,
+        tc.psum_pool(name="psum_q", bufs=1) as psum_q,
+    ):
+        ident = keep.tile([P, P], F32)
+        make_identity(nc, ident[:])
+
+        q_diag = []
+        for turn in range(2):
+            diag = keep.tile([P, BLOCK_T, TILE_PAIRS, 2, ROWS], F32, name="q_diag%d" % turn)
+            nc.gpsimd.memset(diag[:], 0.0)
+            q_diag.append(diag)
+
+        vectors = keep.tile([P, 4, D], BF16)
+        for v, vec in enumerate((lq1, lq2, lk1, lk2)):
+            nc.scalar.dma_start(out=vectors[:, v, :], in_=vec.partition_broadcast(P))
+        lam_products = keep.tile([P, 2, D], F32)
+        nc.vector.tensor_tensor(
+            out=lam_products[:], in0=vectors[:, 0:2, :], in1=vectors[:, 2:4, :], op=ALU.mult
+        )
+        lam_dots = keep.tile([P, 2], F32)
+        nc.vector.tensor_reduce(out=lam_dots[:], in_=lam_products[:], axis=AXIS_X, op=ALU.add)
+        lam_exps = keep.tile([P, 2], F32)
+        nc.scalar.activation(out=lam_exps[:], in_=lam_dots[:], func=ACT.Exp)
+        neg_lam = keep.tile([P, 1], F32)
+        nc.vector.tensor_tensor(
+            out=neg_lam[:], in0=lam_exps[:, 1:2], in1=lam_exps[:, 0:1], op=ALU.subtract
+        )
+        nc.vector.tensor_scalar_add(out=neg_lam[:], in0=neg_lam[:], scalar1=-LAM_INIT)
+        parity = keep.tile([P, 2], F32)
+        nc.vector.tensor_reduce(
+            out=parity[:],
+            in_=ident[:].rearrange("p (c j) -> p j c", j=2),
+            axis=AXIS_X,
+            op=ALU.add,
+        )
+        odd_neg_lam = keep.tile([P, 1], F32)
+        nc.vector.tensor_tensor(out=odd_neg_lam[:], in0=parity[:, 1:2], in1=neg_lam[:], op=ALU.mult)
+
+        w_codes = []
+        w_scales = []
+        for name, W in (("q", Wq), ("k", Wk)):
+            w_sb = stage.tile([P, HEADS * C], BF16, tag="loaded", bufs=3)
+            nc.sync.dma_start(
+                out=w_sb[:].rearrange("p (a c) -> p a c", c=C),
+                in_=W.rearrange("(a p) c -> p a c", p=P),
+            )
+            w_f32 = w_sb[:].bitcast(F32)
+            codes = keep.tile([P, PADDED_ALL], U32, name="codes_" + name, align_bytes=64)
+            scales = keep.tile([P, PADDED_ALL], U8, name="scales_" + name, align_bytes=64)
+            nc.vector.memset(codes[:, PADDED:].bitcast(I32), 0)
+            nc.vector.memset(scales[:, PADDED:].bitcast(I32), 0)
+            for part in range(2):
+                grouped = stage.tile([P, 4 * PADDED // 2], BF16, tag="grouped", align_bytes=64)
+                grouped_words = grouped[:].bitcast(F32)
+                nc.vector.memset(grouped_words, 0.0)
+                by_row = grouped_words.rearrange(
+                    "p (a j z d u) -> p a j z d u", a=HEADS // 2, j=2, z=2, d=D
+                )
+                for a0 in range(0, HEADS // 2, 2):
+                    first = (part * (HEADS // 2) + a0) * WORDS
+                    planes = transpose_words(nc, psum_t, ident, w_f32[:, first : first + 2 * WORDS], 2)
+                    by_j = planes[:].rearrange("p u (a d j) -> p j a d u", a=2, j=2)
+                    for j in range(2):
+                        nc.scalar.copy(out=by_row[:, a0 : a0 + 2, j, 1], in_=by_j[:, j])
+                cols = slice(part * PADDED // 2, (part + 1) * PADDED // 2)
+                nc.vector.quantize_mx(
+                    out=codes[:, cols].bitcast(FP8X4), scales=scales[:, cols], in_=grouped[:]
+                )
+            w_codes.append(codes)
+            w_scales.append(scales)
+
+        x_codes = keep.tile([P, TOKENS], U32, align_bytes=64)
+        x_scales = keep.tile([P, TOKENS], U8, align_bytes=64)
+        for g in [GROUPS - 1] + list(range(TENSOR_GROUPS)):
+            x_sb = stage.tile([P, GROUP_TILES * C], BF16, tag="loaded", bufs=3)
+            nc.sync.dma_start(
+                out=x_sb[:].rearrange("p (y c) -> p y c", c=C),
+                in_=x_rows[g * GROUP_TOKENS : (g + 1) * GROUP_TOKENS, :].rearrange(
+                    "(y p) c -> p y c", p=P
+                ),
+            )
+            x_f32 = x_sb[:].bitcast(F32)
+            grouped = stage.tile([P, 4 * GROUP_TOKENS], BF16, tag="grouped", align_bytes=64)
+            in_order = grouped[:].bitcast(F32).rearrange("p (w u) -> p w u", u=2)
+            by_block = grouped[:].bitcast(F32).rearrange(
+                "p (b s n t u) -> p b s n t u", b=BLOCKS, s=2, n=TILE_PAIRS, u=2
+            )
+            for n in range(TILE_PAIRS):
+                planes = transpose_words(
+                    nc, psum_t, ident, x_f32[:, 2 * n * WORDS : (2 * n + 2) * WORDS], 2
+                )
+                if g < TENSOR_GROUPS:
+                    for s in range(2):
+                        nc.scalar.copy(
+                            out=by_block[:, :, s, n],
+                            in_=planes[:, :, s * P : (s + 1) * P].rearrange(
+                                "p u (b t) -> p b t u", b=BLOCKS
+                            ),
+                        )
+                else:
+                    nc.scalar.copy(
+                        out=in_order[:, 2 * n * P : (2 * n + 2) * P, :],
+                        in_=planes[:].rearrange("p u w -> p w u"),
+                    )
+            cols = slice(g * GROUP_TOKENS, (g + 1) * GROUP_TOKENS)
+            nc.vector.quantize_mx(
+                out=x_codes[:, cols].bitcast(FP8X4), scales=x_scales[:, cols], in_=grouped[:]
+            )
+
+        def project_pairs(w, bank_index, first_token):
+            bank = psum_y.tile([P, BANK_ROWS, P], F32, tag="y")
+            for i in range(BANK_ROWS):
+                r = bank_index * BANK_ROWS + i
+                for s in range(2):
+                    w_cols = slice(P * r + D * (1 - s), P * r + D * (1 - s) + P)
+                    x_cols = slice(first_token + s * P, first_token + (s + 1) * P)
+                    nc.tensor.matmul_mx(
+                        out=bank[:, i, :],
+                        lhsT=w_codes[w][:, w_cols].bitcast(FP8X4),
+                        lhsT_scale=w_scales[w][:, w_cols],
+                        rhs=x_codes[:, x_cols].bitcast(FP8X4),
+                        rhs_scale=x_scales[:, x_cols],
+                        start=(s == 0),
+                        stop=(s == 1),
+                    )
+            return bank
+
+        def score_block(g, b, diag, dense):
+            first_token = g * GROUP_TOKENS + b * BLOCK_TOKENS
+            for bank_index in range(ROWS // BANK_ROWS):
+                rows = slice(bank_index * BANK_ROWS, (bank_index + 1) * BANK_ROWS)
+                bank = project_pairs(0, bank_index, first_token)
+                for s in range(2):
+                    half = slice(s * HALF, (s + 1) * HALF)
+                    nc.scalar.copy(
+                        out=diag[half, :, :, s, rows],
+                        in_=bank[half].rearrange("p i (n t) -> p t n i", n=TILE_PAIRS),
+                    )
+            k_pairs = tensor_way.tile([P, BLOCK_T, ROWS, TILE_PAIRS], F32, bufs=2)
+            for bank_index in range(ROWS // BANK_ROWS):
+                rows = slice(bank_index * BANK_ROWS, (bank_index + 1) * BANK_ROWS)
+                bank = project_pairs(1, bank_index, first_token)
+                nc.scalar.copy(
+                    out=k_pairs[:, :, rows, :],
+                    in_=bank[:].rearrange("p i (n t) -> p t i n", n=TILE_PAIRS),
+                )
+            for t0 in range(0, BLOCK_T, BANK_MATMULS):
+                raw = psum_s.tile([P, BANK_MATMULS, SCORE_COLS], F32, tag="raw")
+                for i in range(BANK_MATMULS):
+                    nc.tensor.matmul(
+                        out=raw[:, i, :],
+                        lhsT=diag[:, t0 + i].rearrange("p n s r -> p (n s r)"),
+                        rhs=k_pairs[:, t0 + i].rearrange("p m n -> p (m n)"),
+                        start=True,
+                        stop=True,
+                    )
+                for n in range(TILE_PAIRS):
+                    quad = slice(n * QUADRANT, (n + 1) * QUADRANT)
+                    first = b * BLOCK_T + t0
+                    nc.scalar.copy(
+                        out=dense[quad, first : first + BANK_MATMULS, :],
+                        in_=raw[quad].rearrange("p i (m n) -> p i m n", n=TILE_PAIRS)[:, :, :, n],
+                    )
+
+        def finish_group(g, dense):
+            dense_shape = [P, P, ROWS]
+            row_max = tensor_way.tile([P, P], F32)
+            nc.vector.tensor_reduce(out=row_max[:], in_=dense[:], axis=AXIS_X, op=ALU.max)
+            nc.vector.tensor_tensor(
+                out=dense[:],
+                in0=dense[:],
+                in1=row_max[:].unsqueeze(2).to_broadcast(dense_shape),
+                op=ALU.subtract,
+            )
+            nc.scalar.activation(out=dense[:], in_=dense[:], func=ACT.Exp, scale=SCALE)
+            row_sum = tensor_way.tile([P, P], F32)
+            nc.vector.tensor_reduce(out=row_sum[:], in_=dense[:], axis=AXIS_X, op=ALU.add)
+            inverse = tensor_way.tile([P, P], F32)
+            nc.vector.reciprocal(out=inverse[:], in_=row_sum[:])
+            by_parity = dense[:].rearrange("p t (h j) -> p j h t", j=2)
+            odd_part = tensor_way.tile([P, HEADS, P], F32)
+            nc.scalar.activation(
+                out=odd_part[:], in_=by_parity[:, 1], func=ACT.Copy, scale=odd_neg_lam[:, 0:1]
+            )
+            picked = tensor_way.tile([P, HEADS, P], F32)
+            nc.vector.scalar_tensor_tensor(
+                out=picked[:],
+                in0=by_parity[:, 0],
+                scalar=parity[:, 0:1],
+                in1=odd_part[:],
+                op0=ALU.mult,
+                op1=ALU.add,
+            )
+            nc.vector.tensor_tensor(
+                out=picked[:],
+                in0=picked[:],
+                in1=inverse[:].unsqueeze(1).to_broadcast([P, HEADS, P]),
+                op=ALU.mult,
+            )
+            result = tensor_way.tile([P, GROUP_TILES, HEADS, HEADS], F32)
+            result_rows = result[:].rearrange("p y a h -> p (y a) h")
+            for h0 in range(0, HEADS, BANK_ROWS):
+                flipped = psum_t.tile([P, BANK_ROWS, P], F32, tag="planes")
+                for i in range(BANK_ROWS):
+                    nc.tensor.transpose(flipped[:, i, :], picked[:, h0 + i, :], ident[:])
+                nc.vector.tensor_reduce(
+                    out=result_rows[:, :, h0 : h0 + BANK_ROWS],
+                    in_=flipped[:].rearrange("p i (e j) -> p e i j", j=2),
+                    axis=AXIS_X,
+                    op=ALU.add,
+                )
+            nc.sync.dma_start(
+                out=out_rows[g * GROUP_TOKENS : (g + 1) * GROUP_TOKENS, :].rearrange(
+                    "(y p) e -> p y e", p=P
+                ),
+                in_=result[:].rearrange("p y a h -> p y (a h)"),
+            )
+
+        def project_tile(w, bank_index, tok, pool, tag):
+            bank = pool.tile([P, BANK], F32, tag=tag)
+            w_cols = slice(D + bank_index * BANK, D + (bank_index + 1) * BANK)
+            nc.tensor.matmul_mx(
+                out=bank[:],
+                lhsT=x_codes[:, tok].bitcast(FP8X4),
+                lhsT_scale=x_scales[:, tok],
+                rhs=w_codes[w][:, w_cols].bitcast(FP8X4),
+                rhs_scale=w_scales[w][:, w_cols],
+                start=True,
+                stop=True,
+            )
+            return bank[:].rearrange("p (i z d) -> p i z d", z=2, d=D)[:, :, 0, :]
+
+        def score_tile(tile_index, scores):
+            tok = slice(tile_index * P, (tile_index + 1) * P)
+            q_psum = project_tile(0, 0, tok, psum_q, "q")
+            q_sb = vector_way.tile([P, ROWS, D], F32)
+            k_sb = vector_way.tile([P, ROWS, D], F32)
+            for bank_index in range(ROWS // BANK_ROWS):
+                rows = slice(bank_index * BANK_ROWS, (bank_index + 1) * BANK_ROWS)
+                nc.scalar.copy(out=k_sb[:, rows, :], in_=project_tile(1, bank_index, tok, psum_y, "y"))
+                if bank_index > 0:
+                    nc.scalar.copy(
+                        out=q_sb[:, rows, :], in_=project_tile(0, bank_index, tok, psum_y, "y")
+                    )
+            chunk_shape = [P, CHUNK_ROWS, ROWS, D]
+            for r0 in range(0, ROWS, CHUNK_ROWS):
+                rows = slice(r0, r0 + CHUNK_ROWS)
+                prod = products.tile(chunk_shape, F32)
+                if r0 < VECTOR_ROWS:
+                    q_chunk = q_psum[:, rows, :]
+                    engine = nc.vector
+                else:
+                    q_chunk = q_sb[:, rows, :]
+                    engine = nc.gpsimd
+                engine.tensor_tensor(
+                    out=prod[:],
+                    in0=q_chunk.unsqueeze(2).to_broadcast(chunk_shape),
+                    in1=k_sb[:].unsqueeze(1).to_broadcast(chunk_shape),
+                    op=ALU.mult,
+                )
+                nc.vector.tensor_reduce(out=scores[:, rows, :], in_=prod[:], axis=AXIS_X, op=ALU.add)
+
+        def finish_batch(first_tile, batch):
+            batch_rows = BATCH_TILES * ROWS
+            batch_shape = [P, batch_rows, ROWS]
+            row_max = vector_way.tile([P, batch_rows], F32)
+            nc.vector.tensor_reduce(out=row_max[:], in_=batch[:], axis=AXIS_X, op=ALU.max)
+            nc.vector.tensor_tensor(
+                out=batch[:],
+                in0=batch[:],
+                in1=row_max[:].unsqueeze(2).to_broadcast(batch_shape),
+                op=ALU.subtract,
+            )
+            nc.scalar.activation(out=batch[:], in_=batch[:], func=ACT.Exp, scale=SCALE)
+            row_sum = vector_way.tile([P, batch_rows], F32)
+            nc.vector.tensor_reduce(out=row_sum[:], in_=batch[:], axis=AXIS_X, op=ALU.add)
+            factor = vector_way.tile([P, batch_rows], F32)
+            nc.vector.reciprocal(out=factor[:], in_=row_sum[:])
+            odd_rows = factor[:].rearrange("p (e j) -> p e j", j=2)[:, :, 1]
+            nc.vector.tensor_scalar_mul(out=odd_rows, in0=odd_rows, scalar1=neg_lam[:, 0:1])
+            nc.vector.tensor_tensor(
+                out=batch[:],
+                in0=batch[:],
+                in1=factor[:].unsqueeze(2).to_broadcast(batch_shape),
+                op=ALU.mult,
+            )
+            by_parity = batch[:].rearrange("p (e j) (h i) -> p e j h i", j=2, i=2)
+            result = vector_way.tile([P, BATCH_TILES * HEADS, HEADS], F32)
+            nc.vector.tensor_tensor(
+                out=result[:], in0=by_parity[:, :, 0, :, 0], in1=by_parity[:, :, 1, :, 1], op=ALU.add
+            )
+            nc.sync.dma_start(
+                out=out_rows[first_tile * P : (first_tile + BATCH_TILES) * P, :].rearrange(
+                    "(y p) e -> p y e", p=P
+                ),
+                in_=result[:].rearrange("p (y a) h -> p y (a h)", a=HEADS),
+            )
+
+        vector_tile = 0
+        for step in range(TENSOR_GROUPS * BLOCKS):
+            g = step // BLOCKS
+            b = step % BLOCKS
+            if step % 3 < 2:
+                if vector_tile % BATCH_TILES == 0:
+                    batch = vector_way.tile([P, BATCH_TILES * ROWS, ROWS], F32)
+                i = vector_tile % BATCH_TILES
+                score_tile(
+                    TENSOR_GROUPS * GROUP_TILES + vector_tile, batch[:, i * ROWS : (i + 1) * ROWS, :]
+                )
+                vector_tile += 1
+                if vector_tile % BATCH_TILES == 0:
+                    finish_batch(TENSOR_GROUPS * GROUP_TILES + vector_tile - BATCH_TILES, batch)
+            if b == 0:
+                dense = tensor_way.tile([P, P, ROWS], F32, bufs=2)
+            score_block(g, b, q_diag[step % 2], dense)
+            if b == BLOCKS - 1:
+                finish_group(g, dense)

@@ -20,6 +20,7 @@ TOKENS = 4 * 1024
 C = 512
 WORDS = C // 2
 ROWS = 16
+DIFFS = ROWS - 1
 D = 64
 HEADS = 8
 BANK = 512
@@ -27,23 +28,34 @@ BANK_ROWS = 4
 SCALE = D ** -0.5
 LAM_INIT = 0.8 - 0.6 * math.exp(-0.3 * 12)
 
-GROUP_TILES = 8
-GROUP_TOKENS = GROUP_TILES * P
+RUNS = 8
+PAIRS = RUNS // 2
+GROUP_TOKENS = P * RUNS
 GROUPS = TOKENS // GROUP_TOKENS
-TENSOR_GROUPS = 3
-TILE_PAIRS = GROUP_TILES // 2
-BLOCKS = 4
-BLOCK_T = P // BLOCKS
-BLOCK_TOKENS = GROUP_TILES * BLOCK_T
-SCORE_COLS = ROWS * TILE_PAIRS
-BANK_MATMULS = BANK // SCORE_COLS
+FULL_GROUPS = 3
+BLOCK_T = 32
+GROUP_BLOCKS = P // BLOCK_T
+BLOCK_TOKENS = BLOCK_T * RUNS
+HALF_T = 16
+LAST_T = BLOCK_T + HALF_T
+TENSOR_T = FULL_GROUPS * P + LAST_T
+BLOCKS = FULL_GROUPS * GROUP_BLOCKS + 2
+VECTOR_T = P - LAST_T
+VECTOR_TILES = VECTOR_T * RUNS // P
+
+LAST_COL = FULL_GROUPS * GROUP_TOKENS
+HALF_COL = LAST_COL + BLOCK_TOKENS
+VECTOR_COL = HALF_COL + BLOCK_TOKENS
+X_COLS = VECTOR_COL + VECTOR_TILES * P
+
+SCORE_COLS = DIFFS * PAIRS
+BANK_MATMULS = 8
 
 PADDED = 2 * ROWS * D
 PADDED_ALL = PADDED + D
 
-CHUNK_ROWS = 2
-VECTOR_ROWS = BANK_ROWS
-BATCH_TILES = 4
+VECTOR_ROWS = 2
+SUM_LAG = 2
 
 FLOPS = 2 * TOKENS * C * 2 * ROWS * D + 2 * TOKENS * ROWS * ROWS * D
 
@@ -70,7 +82,7 @@ def tile_differentialattention_pa_t_kernel(tc, x, Wq, Wk, lq1, lq2, lk1, lk2, ou
         tc.tile_pool(name="stage", bufs=2) as stage,
         tc.tile_pool(name="tensor_way", bufs=1) as tensor_way,
         tc.tile_pool(name="vector_way", bufs=2) as vector_way,
-        tc.tile_pool(name="products", bufs=4) as products,
+        tc.tile_pool(name="products", bufs=6) as products,
         tc.psum_pool(name="psum_t", bufs=2) as psum_t,
         tc.psum_pool(name="psum_y", bufs=3) as psum_y,
         tc.psum_pool(name="psum_s", bufs=2) as psum_s,
@@ -79,15 +91,132 @@ def tile_differentialattention_pa_t_kernel(tc, x, Wq, Wk, lq1, lq2, lk1, lk2, ou
         ident = keep.tile([P, P], F32)
         make_identity(nc, ident[:])
 
+        dense_flat = keep.tile([P, TENSOR_T * DIFFS], F32, align_bytes=64)
+        dense = dense_flat[:].rearrange("p (t m) -> p t m", m=DIFFS)
+        w_grouped = []
+        for turn in range(2):
+            words = dense_flat[:, turn * PADDED : (turn + 1) * PADDED]
+            nc.gpsimd.memset(words, 0.0)
+            w_grouped.append(words)
+
         q_diag = []
         for turn in range(2):
-            diag = keep.tile([P, BLOCK_T, TILE_PAIRS, 2, ROWS], F32, name="q_diag%d" % turn)
+            diag = keep.tile([P, BLOCK_T, PAIRS, 2, ROWS], F32, name="q_diag%d" % turn)
             nc.gpsimd.memset(diag[:], 0.0)
             q_diag.append(diag)
 
+        def copy_out(index, **operands):
+            if index % 2 == 0:
+                nc.scalar.copy(**operands)
+            else:
+                nc.vector.tensor_copy(**operands)
+
+        w_codes = {}
+        w_scales = {}
+        for w, W in ((1, Wk), (0, Wq)):
+            codes = keep.tile([P, PADDED_ALL], U32, name="codes_%d" % w, align_bytes=64)
+            scales = keep.tile([P, PADDED_ALL], U8, name="scales_%d" % w, align_bytes=64)
+            nc.vector.memset(codes[:, PADDED:].bitcast(I32), 0)
+            nc.vector.memset(scales[:, PADDED:].bitcast(I32), 0)
+            for part in range(2):
+                w_sb = stage.tile([P, HEADS // 2 * C], BF16, tag="loaded", bufs=3)
+                nc.sync.dma_start(
+                    out=w_sb[:].rearrange("p (a c) -> p a c", c=C),
+                    in_=W[part * 512 : (part + 1) * 512, :].rearrange("(a p) c -> p a c", p=P),
+                )
+                w_f32 = w_sb[:].bitcast(F32)
+                grouped = w_grouped[part]
+                by_row = grouped.rearrange(
+                    "p (a j z d u) -> p a j z d u", a=HEADS // 2, j=2, z=2, d=D
+                )
+                for a0 in range(0, HEADS // 2, 2):
+                    planes = transpose_words(
+                        nc, psum_t, ident, w_f32[:, a0 * WORDS : (a0 + 2) * WORDS], 2
+                    )
+                    by_j = planes[:].rearrange("p u (a d j) -> p j a d u", a=2, j=2)
+                    for j in range(2):
+                        copy_out(a0 // 2, out=by_row[:, a0 : a0 + 2, j, 1], in_=by_j[:, j])
+                cols = slice(part * PADDED // 2, (part + 1) * PADDED // 2)
+                nc.vector.quantize_mx(
+                    out=codes[:, cols].bitcast(FP8X4), scales=scales[:, cols], in_=grouped.bitcast(BF16)
+                )
+            w_codes[w] = codes
+            w_scales[w] = scales
+
+        x_codes = keep.tile([P, X_COLS], U32, align_bytes=64)
+        x_scales = keep.tile([P, X_COLS], U8, align_bytes=64)
+
+        def quantise_x(first, grouped):
+            cols = slice(first, first + grouped.shape[1] // 4)
+            nc.vector.quantize_mx(
+                out=x_codes[:, cols].bitcast(FP8X4), scales=x_scales[:, cols], in_=grouped
+            )
+
+        x_words = {}
+        for g in [GROUPS - 1] + list(range(FULL_GROUPS)):
+            x_sb = stage.tile([P, RUNS * C], BF16, tag="loaded", bufs=3)
+            nc.sync.dma_start(
+                out=x_sb[:],
+                in_=x_rows[g * GROUP_TOKENS : (g + 1) * GROUP_TOKENS, :].rearrange(
+                    "(t y) c -> t (y c)", y=RUNS
+                ),
+            )
+            x_words[g] = x_sb[:].bitcast(F32)
+
+        def prepare_last_group():
+            last = stage.tile([P, 4 * 2 * BLOCK_TOKENS], BF16, tag="grouped", align_bytes=64)
+            last_words = last[:].bitcast(F32)
+            by_half = last_words[:, : 2 * BLOCK_TOKENS].rearrange(
+                "p (s n t u) -> p s n t u", s=2, n=PAIRS, u=2
+            )
+            short = last_words[:, 2 * BLOCK_TOKENS :].rearrange(
+                "p (i s n t u) -> p i s n t u", i=2, s=2, n=PAIRS, u=2
+            )
+            vec = stage.tile([P, 4 * VECTOR_TILES * P], BF16, tag="vec", bufs=1, align_bytes=64)
+            by_run = vec[:].bitcast(F32).rearrange("p (y t u) -> p y t u", y=RUNS, u=2)
+            for n in range(PAIRS):
+                planes = transpose_words(
+                    nc, psum_t, ident, x_words[GROUPS - 1][:, 2 * n * WORDS : (2 * n + 2) * WORDS], 2
+                )
+                by_time = planes[:].rearrange("p u (s t) -> p s t u", s=2)
+                copy_out(n, out=by_run[:, 2 * n : 2 * n + 2], in_=by_time[:, :, LAST_T:, :])
+                copy_out(n, out=by_half[:, :, n], in_=by_time[:, :, :BLOCK_T, :])
+                for i in range(2):
+                    copy_out(n, out=short[:, i, :, n], in_=by_time[:, :, BLOCK_T:LAST_T, :])
+            for first, tiles in ((0, 2), (2, 2), (4, 1)):
+                quantise_x(VECTOR_COL + first * P, vec[:, 4 * first * P : 4 * (first + tiles) * P])
+            quantise_x(LAST_COL, last[:])
+
+        def full_group_pieces(g):
+            grouped = stage.tile([P, 4 * GROUP_TOKENS], BF16, tag="grouped", align_bytes=64)
+            by_block = grouped[:].bitcast(F32).rearrange(
+                "p (b s n t u) -> p b s n t u", b=GROUP_BLOCKS, s=2, n=PAIRS, u=2
+            )
+
+            def turn_pair(n):
+                planes = transpose_words(
+                    nc, psum_t, ident, x_words[g][:, 2 * n * WORDS : (2 * n + 2) * WORDS], 2
+                )
+                for s in range(2):
+                    copy_out(
+                        n,
+                        out=by_block[:, :, s, n],
+                        in_=planes[:, :, s * P : (s + 1) * P].rearrange(
+                            "p u (b t) -> p b t u", b=GROUP_BLOCKS
+                        ),
+                    )
+
+            pieces = [lambda n=n: turn_pair(n) for n in range(PAIRS)]
+            pieces.append(lambda: quantise_x(g * GROUP_TOKENS, grouped[:]))
+            return pieces
+
+        prepare_last_group()
+        for piece in full_group_pieces(0):
+            piece()
+
         vectors = keep.tile([P, 4, D], BF16)
-        for v, vec in enumerate((lq1, lq2, lk1, lk2)):
-            nc.scalar.dma_start(out=vectors[:, v, :], in_=vec.partition_broadcast(P))
+        for v, vector in enumerate((lq1, lq2, lk1, lk2)):
+            nc.sync.dma_start(out=vectors[:, v, :], in_=vector.partition_broadcast(P))
         lam_products = keep.tile([P, 2, D], F32)
         nc.vector.tensor_tensor(
             out=lam_products[:], in0=vectors[:, 0:2, :], in1=vectors[:, 2:4, :], op=ALU.mult
@@ -101,94 +230,16 @@ def tile_differentialattention_pa_t_kernel(tc, x, Wq, Wk, lq1, lq2, lk1, lk2, ou
             out=neg_lam[:], in0=lam_exps[:, 1:2], in1=lam_exps[:, 0:1], op=ALU.subtract
         )
         nc.vector.tensor_scalar_add(out=neg_lam[:], in0=neg_lam[:], scalar1=-LAM_INIT)
-        parity = keep.tile([P, 2], F32)
-        nc.vector.tensor_reduce(
-            out=parity[:],
-            in_=ident[:].rearrange("p (c j) -> p j c", j=2),
-            axis=AXIS_X,
-            op=ALU.add,
-        )
-        odd_neg_lam = keep.tile([P, 1], F32)
-        nc.vector.tensor_tensor(out=odd_neg_lam[:], in0=parity[:, 1:2], in1=neg_lam[:], op=ALU.mult)
 
-        w_codes = []
-        w_scales = []
-        for name, W in (("q", Wq), ("k", Wk)):
-            w_sb = stage.tile([P, HEADS * C], BF16, tag="loaded", bufs=3)
-            nc.sync.dma_start(
-                out=w_sb[:].rearrange("p (a c) -> p a c", c=C),
-                in_=W.rearrange("(a p) c -> p a c", p=P),
-            )
-            w_f32 = w_sb[:].bitcast(F32)
-            codes = keep.tile([P, PADDED_ALL], U32, name="codes_" + name, align_bytes=64)
-            scales = keep.tile([P, PADDED_ALL], U8, name="scales_" + name, align_bytes=64)
-            nc.vector.memset(codes[:, PADDED:].bitcast(I32), 0)
-            nc.vector.memset(scales[:, PADDED:].bitcast(I32), 0)
-            for part in range(2):
-                grouped = stage.tile([P, 4 * PADDED // 2], BF16, tag="grouped", align_bytes=64)
-                grouped_words = grouped[:].bitcast(F32)
-                nc.vector.memset(grouped_words, 0.0)
-                by_row = grouped_words.rearrange(
-                    "p (a j z d u) -> p a j z d u", a=HEADS // 2, j=2, z=2, d=D
-                )
-                for a0 in range(0, HEADS // 2, 2):
-                    first = (part * (HEADS // 2) + a0) * WORDS
-                    planes = transpose_words(nc, psum_t, ident, w_f32[:, first : first + 2 * WORDS], 2)
-                    by_j = planes[:].rearrange("p u (a d j) -> p j a d u", a=2, j=2)
-                    for j in range(2):
-                        nc.scalar.copy(out=by_row[:, a0 : a0 + 2, j, 1], in_=by_j[:, j])
-                cols = slice(part * PADDED // 2, (part + 1) * PADDED // 2)
-                nc.vector.quantize_mx(
-                    out=codes[:, cols].bitcast(FP8X4), scales=scales[:, cols], in_=grouped[:]
-                )
-            w_codes.append(codes)
-            w_scales.append(scales)
+        neg_max = keep.tile([P, TENSOR_T], F32)
 
-        x_codes = keep.tile([P, TOKENS], U32, align_bytes=64)
-        x_scales = keep.tile([P, TOKENS], U8, align_bytes=64)
-        for g in [GROUPS - 1] + list(range(TENSOR_GROUPS)):
-            x_sb = stage.tile([P, GROUP_TILES * C], BF16, tag="loaded", bufs=3)
-            nc.sync.dma_start(
-                out=x_sb[:].rearrange("p (y c) -> p y c", c=C),
-                in_=x_rows[g * GROUP_TOKENS : (g + 1) * GROUP_TOKENS, :].rearrange(
-                    "(y p) c -> p y c", p=P
-                ),
-            )
-            x_f32 = x_sb[:].bitcast(F32)
-            grouped = stage.tile([P, 4 * GROUP_TOKENS], BF16, tag="grouped", align_bytes=64)
-            in_order = grouped[:].bitcast(F32).rearrange("p (w u) -> p w u", u=2)
-            by_block = grouped[:].bitcast(F32).rearrange(
-                "p (b s n t u) -> p b s n t u", b=BLOCKS, s=2, n=TILE_PAIRS, u=2
-            )
-            for n in range(TILE_PAIRS):
-                planes = transpose_words(
-                    nc, psum_t, ident, x_f32[:, 2 * n * WORDS : (2 * n + 2) * WORDS], 2
-                )
-                if g < TENSOR_GROUPS:
-                    for s in range(2):
-                        nc.scalar.copy(
-                            out=by_block[:, :, s, n],
-                            in_=planes[:, :, s * P : (s + 1) * P].rearrange(
-                                "p u (b t) -> p b t u", b=BLOCKS
-                            ),
-                        )
-                else:
-                    nc.scalar.copy(
-                        out=in_order[:, 2 * n * P : (2 * n + 2) * P, :],
-                        in_=planes[:].rearrange("p u w -> p w u"),
-                    )
-            cols = slice(g * GROUP_TOKENS, (g + 1) * GROUP_TOKENS)
-            nc.vector.quantize_mx(
-                out=x_codes[:, cols].bitcast(FP8X4), scales=x_scales[:, cols], in_=grouped[:]
-            )
-
-        def project_pairs(w, bank_index, first_token):
+        def project_pairs(w, bank_index, first_cols):
             bank = psum_y.tile([P, BANK_ROWS, P], F32, tag="y")
             for i in range(BANK_ROWS):
                 r = bank_index * BANK_ROWS + i
                 for s in range(2):
                     w_cols = slice(P * r + D * (1 - s), P * r + D * (1 - s) + P)
-                    x_cols = slice(first_token + s * P, first_token + (s + 1) * P)
+                    x_cols = slice(first_cols[s], first_cols[s] + P)
                     nc.tensor.matmul_mx(
                         out=bank[:, i, :],
                         lhsT=w_codes[w][:, w_cols].bitcast(FP8X4),
@@ -200,99 +251,146 @@ def tile_differentialattention_pa_t_kernel(tc, x, Wq, Wk, lq1, lq2, lk1, lk2, ou
                     )
             return bank
 
-        def score_block(g, b, diag, dense):
-            first_token = g * GROUP_TOKENS + b * BLOCK_TOKENS
-            for bank_index in range(ROWS // BANK_ROWS):
-                rows = slice(bank_index * BANK_ROWS, (bank_index + 1) * BANK_ROWS)
-                bank = project_pairs(0, bank_index, first_token)
-                for s in range(2):
-                    half = slice(s * HALF, (s + 1) * HALF)
-                    nc.scalar.copy(
-                        out=diag[half, :, :, s, rows],
-                        in_=bank[half].rearrange("p i (n t) -> p t n i", n=TILE_PAIRS),
-                    )
-            k_pairs = tensor_way.tile([P, BLOCK_T, ROWS, TILE_PAIRS], F32, bufs=2)
-            for bank_index in range(ROWS // BANK_ROWS):
-                rows = slice(bank_index * BANK_ROWS, (bank_index + 1) * BANK_ROWS)
-                bank = project_pairs(1, bank_index, first_token)
-                nc.scalar.copy(
-                    out=k_pairs[:, :, rows, :],
-                    in_=bank[:].rearrange("p i (n t) -> p t i n", n=TILE_PAIRS),
-                )
-            for t0 in range(0, BLOCK_T, BANK_MATMULS):
-                raw = psum_s.tile([P, BANK_MATMULS, SCORE_COLS], F32, tag="raw")
-                for i in range(BANK_MATMULS):
-                    nc.tensor.matmul(
-                        out=raw[:, i, :],
-                        lhsT=diag[:, t0 + i].rearrange("p n s r -> p (n s r)"),
-                        rhs=k_pairs[:, t0 + i].rearrange("p m n -> p (m n)"),
-                        start=True,
-                        stop=True,
-                    )
-                for n in range(TILE_PAIRS):
-                    quad = slice(n * QUADRANT, (n + 1) * QUADRANT)
-                    first = b * BLOCK_T + t0
-                    nc.scalar.copy(
-                        out=dense[quad, first : first + BANK_MATMULS, :],
-                        in_=raw[quad].rearrange("p i (m n) -> p i m n", n=TILE_PAIRS)[:, :, :, n],
-                    )
+        def block_times(block):
+            return BLOCK_T if block < BLOCKS - 1 else HALF_T
 
-        def finish_group(g, dense):
-            dense_shape = [P, P, ROWS]
-            row_max = tensor_way.tile([P, P], F32)
-            nc.vector.tensor_reduce(out=row_max[:], in_=dense[:], axis=AXIS_X, op=ALU.max)
+        def open_block(block):
+            k_pairs = tensor_way.tile([P, BLOCK_T, DIFFS, PAIRS], F32, bufs=2)
+            k_first = tensor_way.tile([P, BLOCK_T, PAIRS], F32, bufs=2)
+            return q_diag[block % 2], k_pairs, k_first
+
+        def project_step(block, operands, bank_index):
+            diag, k_pairs, k_first = operands
+            times = block_times(block)
+            if block < BLOCKS - 1:
+                first_cols = (block * BLOCK_TOKENS, block * BLOCK_TOKENS + P)
+            else:
+                first_cols = (HALF_COL, HALF_COL + HALF)
+            rows = slice(bank_index * BANK_ROWS, (bank_index + 1) * BANK_ROWS)
+            bank = project_pairs(1, bank_index, first_cols)
+            by_time = bank[:, :, : PAIRS * times].rearrange("p i (n t) -> p t i n", n=PAIRS)
+            skip = 1 if bank_index == 0 else 0
+            if skip:
+                nc.scalar.copy(out=k_first[:, :times], in_=by_time[:, :, 0])
+            first = bank_index * BANK_ROWS + skip - 1
+            count = BANK_ROWS - skip
             nc.vector.tensor_tensor(
-                out=dense[:],
-                in0=dense[:],
-                in1=row_max[:].unsqueeze(2).to_broadcast(dense_shape),
+                out=k_pairs[:, :times, first : first + count, :],
+                in0=by_time[:, :, skip:],
+                in1=k_first[:, :times].unsqueeze(2).to_broadcast([P, times, count, PAIRS]),
                 op=ALU.subtract,
             )
-            nc.scalar.activation(out=dense[:], in_=dense[:], func=ACT.Exp, scale=SCALE)
-            row_sum = tensor_way.tile([P, P], F32)
-            nc.vector.tensor_reduce(out=row_sum[:], in_=dense[:], axis=AXIS_X, op=ALU.add)
-            inverse = tensor_way.tile([P, P], F32)
-            nc.vector.reciprocal(out=inverse[:], in_=row_sum[:])
-            by_parity = dense[:].rearrange("p t (h j) -> p j h t", j=2)
-            odd_part = tensor_way.tile([P, HEADS, P], F32)
-            nc.scalar.activation(
-                out=odd_part[:], in_=by_parity[:, 1], func=ACT.Copy, scale=odd_neg_lam[:, 0:1]
-            )
-            picked = tensor_way.tile([P, HEADS, P], F32)
-            nc.vector.scalar_tensor_tensor(
-                out=picked[:],
-                in0=by_parity[:, 0],
-                scalar=parity[:, 0:1],
-                in1=odd_part[:],
-                op0=ALU.mult,
-                op1=ALU.add,
-            )
-            nc.vector.tensor_tensor(
-                out=picked[:],
-                in0=picked[:],
-                in1=inverse[:].unsqueeze(1).to_broadcast([P, HEADS, P]),
-                op=ALU.mult,
-            )
-            result = tensor_way.tile([P, GROUP_TILES, HEADS, HEADS], F32)
-            result_rows = result[:].rearrange("p y a h -> p (y a) h")
-            for h0 in range(0, HEADS, BANK_ROWS):
+            bank = project_pairs(0, bank_index, first_cols)
+            for s in range(2):
+                half = slice(s * HALF, (s + 1) * HALF)
+                nc.scalar.copy(
+                    out=diag[half, :times, :, s, rows],
+                    in_=bank[half, :, : PAIRS * times].rearrange("p i (n t) -> p t n i", n=PAIRS),
+                )
+
+        def score_step(block, operands, t0):
+            diag, k_pairs, k_first = operands
+            raw = psum_s.tile([P, BANK_MATMULS, SCORE_COLS], F32, tag="raw")
+            for i in range(BANK_MATMULS):
+                nc.tensor.matmul(
+                    out=raw[:, i, :],
+                    lhsT=diag[:, t0 + i].rearrange("p n s r -> p (n s r)"),
+                    rhs=k_pairs[:, t0 + i].rearrange("p m n -> p (m n)"),
+                    start=True,
+                    stop=True,
+                )
+            first = block * BLOCK_T + t0
+            for n in range(PAIRS):
+                quad = slice(n * QUADRANT, (n + 1) * QUADRANT)
+                nc.scalar.copy(
+                    out=dense[quad, first : first + BANK_MATMULS, :],
+                    in_=raw[quad].rearrange("p i (m n) -> p i m n", n=PAIRS)[:, :, :, n],
+                )
+
+        def finish_pieces(first_new, end, lo):
+            new = slice(first_new, end)
+            first = end - P
+            exps = tensor_way.tile([P, P, ROWS], F32)
+
+            def find_max():
+                nc.vector.tensor_reduce(
+                    out=neg_max[:, new], in_=dense[:, new, :], axis=AXIS_X, op=ALU.max
+                )
+                nc.vector.tensor_scalar(
+                    out=neg_max[:, new], in0=neg_max[:, new], scalar1=-1.0, scalar2=0.0,
+                    op0=ALU.mult, op1=ALU.min,
+                )
+
+            def turn_and_exp(m0):
                 flipped = psum_t.tile([P, BANK_ROWS, P], F32, tag="planes")
                 for i in range(BANK_ROWS):
-                    nc.tensor.transpose(flipped[:, i, :], picked[:, h0 + i, :], ident[:])
-                nc.vector.tensor_reduce(
-                    out=result_rows[:, :, h0 : h0 + BANK_ROWS],
-                    in_=flipped[:].rearrange("p i (e j) -> p e i j", j=2),
-                    axis=AXIS_X,
-                    op=ALU.add,
+                    m = m0 + i
+                    if m > 0:
+                        nc.tensor.matmul(
+                            out=flipped[:, i, :],
+                            lhsT=dense[:, first:end, m - 1],
+                            rhs=ident[:],
+                            start=True,
+                            stop=False,
+                            is_transpose=True,
+                        )
+                    nc.tensor.matmul(
+                        out=flipped[:, i, :],
+                        lhsT=neg_max[:, first:end],
+                        rhs=ident[:],
+                        start=(m == 0),
+                        stop=True,
+                        is_transpose=True,
+                    )
+                nc.scalar.activation(
+                    out=exps[lo:, :, m0 : m0 + BANK_ROWS],
+                    in_=flipped[lo:].rearrange("p i e -> p e i"),
+                    func=ACT.Exp,
+                    scale=SCALE,
                 )
-            nc.sync.dma_start(
-                out=out_rows[g * GROUP_TOKENS : (g + 1) * GROUP_TOKENS, :].rearrange(
-                    "(y p) e -> p y e", p=P
-                ),
-                in_=result[:].rearrange("p y a h -> p y (a h)"),
-            )
 
-        def project_tile(w, bank_index, tok, pool, tag):
+            factor = tensor_way.tile([P, P], F32, bufs=2)
+            by_j = factor[:].rearrange("p (e j) -> p j e", j=2)
+
+            def find_factors():
+                row_sum = tensor_way.tile([P, P], F32, bufs=2)
+                nc.vector.tensor_reduce(out=row_sum[lo:], in_=exps[lo:], axis=AXIS_X, op=ALU.add)
+                nc.vector.reciprocal(out=factor[lo:], in_=row_sum[lo:])
+                nc.vector.tensor_scalar_mul(
+                    out=by_j[lo:, 1], in0=by_j[lo:, 1], scalar1=neg_lam[lo:, 0:1]
+                )
+
+            def combine():
+                by_parity = exps[:].rearrange("p (e j) (h i) -> p j i e h", j=2, i=2)
+                terms = []
+                for j in range(2):
+                    term = tensor_way.tile([P, RUNS * HEADS, HEADS], F32, name="term%d" % j)
+                    nc.vector.tensor_tensor(
+                        out=term[lo:],
+                        in0=by_parity[lo:, j, j],
+                        in1=by_j[lo:, j].unsqueeze(2).to_broadcast([P - lo, RUNS * HEADS, HEADS]),
+                        op=ALU.mult,
+                    )
+                    terms.append(term)
+                result = tensor_way.tile([P, RUNS * HEADS, HEADS], F32)
+                nc.vector.tensor_tensor(
+                    out=result[lo:], in0=terms[0][lo:], in1=terms[1][lo:], op=ALU.add
+                )
+                nc.sync.dma_start(
+                    out=out_rows[first_new * RUNS : end * RUNS, :].rearrange(
+                        "(t y) e -> t (y e)", y=RUNS
+                    ),
+                    in_=result[first_new - first :].rearrange("p e h -> p (e h)"),
+                )
+
+            pieces = [find_max]
+            pieces += [lambda m0=m0: turn_and_exp(m0) for m0 in range(0, ROWS, BANK_ROWS)]
+            pieces += [find_factors, combine]
+            return pieces
+
+        def project_tile(w, bank_index, tile_index, pool, tag):
             bank = pool.tile([P, BANK], F32, tag=tag)
+            tok = slice(VECTOR_COL + tile_index * P, VECTOR_COL + (tile_index + 1) * P)
             w_cols = slice(D + bank_index * BANK, D + (bank_index + 1) * BANK)
             nc.tensor.matmul_mx(
                 out=bank[:],
@@ -305,38 +403,51 @@ def tile_differentialattention_pa_t_kernel(tc, x, Wq, Wk, lq1, lq2, lk1, lk2, ou
             )
             return bank[:].rearrange("p (i z d) -> p i z d", z=2, d=D)[:, :, 0, :]
 
-        def score_tile(tile_index, scores):
-            tok = slice(tile_index * P, (tile_index + 1) * P)
-            q_psum = project_tile(0, 0, tok, psum_q, "q")
+        def open_tile(tile_index):
+            q_psum = project_tile(0, 0, tile_index, psum_q, "q")
             q_sb = vector_way.tile([P, ROWS, D], F32)
-            k_sb = vector_way.tile([P, ROWS, D], F32)
-            for bank_index in range(ROWS // BANK_ROWS):
-                rows = slice(bank_index * BANK_ROWS, (bank_index + 1) * BANK_ROWS)
-                nc.scalar.copy(out=k_sb[:, rows, :], in_=project_tile(1, bank_index, tok, psum_y, "y"))
-                if bank_index > 0:
-                    nc.scalar.copy(
-                        out=q_sb[:, rows, :], in_=project_tile(0, bank_index, tok, psum_y, "y")
-                    )
-            chunk_shape = [P, CHUNK_ROWS, ROWS, D]
-            for r0 in range(0, ROWS, CHUNK_ROWS):
-                rows = slice(r0, r0 + CHUNK_ROWS)
-                prod = products.tile(chunk_shape, F32)
-                if r0 < VECTOR_ROWS:
-                    q_chunk = q_psum[:, rows, :]
-                    engine = nc.vector
-                else:
-                    q_chunk = q_sb[:, rows, :]
-                    engine = nc.gpsimd
-                engine.tensor_tensor(
-                    out=prod[:],
-                    in0=q_chunk.unsqueeze(2).to_broadcast(chunk_shape),
-                    in1=k_sb[:].unsqueeze(1).to_broadcast(chunk_shape),
-                    op=ALU.mult,
-                )
-                nc.vector.tensor_reduce(out=scores[:, rows, :], in_=prod[:], axis=AXIS_X, op=ALU.add)
+            k_sb = vector_way.tile([P, DIFFS, D], F32)
+            k_zero = vector_way.tile([P, D], F32)
+            return q_psum, q_sb, k_sb, k_zero
 
-        def finish_batch(first_tile, batch):
-            batch_rows = BATCH_TILES * ROWS
+        def fill_tile(tile_index, operands, bank_index):
+            q_psum, q_sb, k_sb, k_zero = operands
+            bank = project_tile(1, bank_index, tile_index, psum_y, "y")
+            skip = 1 if bank_index == 0 else 0
+            if skip:
+                nc.scalar.copy(out=k_zero[:], in_=bank[:, 0])
+            first = bank_index * BANK_ROWS + skip - 1
+            count = BANK_ROWS - skip
+            nc.vector.tensor_tensor(
+                out=k_sb[:, first : first + count, :],
+                in0=bank[:, skip:],
+                in1=k_zero[:].unsqueeze(1).to_broadcast([P, count, D]),
+                op=ALU.subtract,
+            )
+            if bank_index == 0:
+                nc.scalar.copy(out=q_sb[:, VECTOR_ROWS:BANK_ROWS, :], in_=q_psum[:, VECTOR_ROWS:])
+            else:
+                nc.scalar.copy(
+                    out=q_sb[:, bank_index * BANK_ROWS : (bank_index + 1) * BANK_ROWS, :],
+                    in_=project_tile(0, bank_index, tile_index, psum_y, "y"),
+                )
+
+        def multiply_row(operands, r):
+            q_psum, q_sb, k_sb, k_zero = operands
+            prod = products.tile([P, DIFFS, D], F32)
+            on_vector = r < VECTOR_ROWS
+            engine = nc.vector if on_vector else nc.gpsimd
+            q_row = q_psum[:, r, :] if on_vector else q_sb[:, r, :]
+            engine.tensor_tensor(
+                out=prod[:],
+                in0=q_row.unsqueeze(1).to_broadcast([P, DIFFS, D]),
+                in1=k_sb[:],
+                op=ALU.mult,
+            )
+            return prod
+
+        def finish_batch(first_tile, tiles, batch):
+            batch_rows = tiles * ROWS
             batch_shape = [P, batch_rows, ROWS]
             row_max = vector_way.tile([P, batch_rows], F32)
             nc.vector.tensor_reduce(out=row_max[:], in_=batch[:], axis=AXIS_X, op=ALU.max)
@@ -360,33 +471,97 @@ def tile_differentialattention_pa_t_kernel(tc, x, Wq, Wk, lq1, lq2, lk1, lk2, ou
                 op=ALU.mult,
             )
             by_parity = batch[:].rearrange("p (e j) (h i) -> p e j h i", j=2, i=2)
-            result = vector_way.tile([P, BATCH_TILES * HEADS, HEADS], F32)
+            result = vector_way.tile([P, tiles * HEADS, HEADS], F32)
             nc.vector.tensor_tensor(
                 out=result[:], in0=by_parity[:, :, 0, :, 0], in1=by_parity[:, :, 1, :, 1], op=ALU.add
             )
-            nc.sync.dma_start(
-                out=out_rows[first_tile * P : (first_tile + BATCH_TILES) * P, :].rearrange(
-                    "(y p) e -> p y e", p=P
-                ),
-                in_=result[:].rearrange("p (y a) h -> p y (a h)", a=HEADS),
-            )
+            by_run = out_rows.rearrange("(t y) e -> y t e", y=RUNS)
+            for v in range(tiles):
+                at = (first_tile + v) * P
+                stop = at + P
+                p0 = 0
+                while at < stop:
+                    y, t = divmod(at, VECTOR_T)
+                    count = min(VECTOR_T - t, stop - at)
+                    nc.sync.dma_start(
+                        out=by_run[y, TENSOR_T + t : TENSOR_T + t + count, :],
+                        in_=result[p0 : p0 + count, v * HEADS : (v + 1) * HEADS, :].rearrange(
+                            "p a h -> p (a h)"
+                        ),
+                    )
+                    at += count
+                    p0 += count
 
-        vector_tile = 0
-        for step in range(TENSOR_GROUPS * BLOCKS):
-            g = step // BLOCKS
-            b = step % BLOCKS
-            if step % 3 < 2:
-                if vector_tile % BATCH_TILES == 0:
-                    batch = vector_way.tile([P, BATCH_TILES * ROWS, ROWS], F32)
-                i = vector_tile % BATCH_TILES
-                score_tile(
-                    TENSOR_GROUPS * GROUP_TILES + vector_tile, batch[:, i * ROWS : (i + 1) * ROWS, :]
-                )
-                vector_tile += 1
-                if vector_tile % BATCH_TILES == 0:
-                    finish_batch(TENSOR_GROUPS * GROUP_TILES + vector_tile - BATCH_TILES, batch)
-            if b == 0:
-                dense = tensor_way.tile([P, P, ROWS], F32, bufs=2)
-            score_block(g, b, q_diag[step % 2], dense)
-            if b == BLOCKS - 1:
-                finish_group(g, dense)
+        BATCHES = ((0, 3), (3, 2))
+        row_order = [2, 3, 0] + list(range(4, 8)) + [1] + list(range(8, ROWS))
+        tiles_open = {}
+        scores_of = {}
+        waiting = []
+
+        def sum_oldest():
+            prod, tile_index, r = waiting.pop(0)
+            nc.vector.tensor_reduce(
+                out=scores_of[tile_index][:, r, 1:], in_=prod[:], axis=AXIS_X, op=ALU.add
+            )
+            if r == row_order[-1]:
+                for first_tile, tiles in BATCHES:
+                    if tile_index == first_tile + tiles - 1:
+                        finish_batch(first_tile, tiles, scores_of["batch", first_tile])
+
+        def open_step(tile_index, bank_index):
+            if bank_index == 0:
+                tiles_open[tile_index] = open_tile(tile_index)
+                for first_tile, tiles in BATCHES:
+                    if tile_index == first_tile:
+                        batch = vector_way.tile([P, tiles * ROWS, ROWS], F32)
+                        nc.vector.memset(batch[:, :, 0:1], 0.0)
+                        scores_of["batch", first_tile] = batch
+                        for v in range(tiles):
+                            scores_of[first_tile + v] = batch[:, v * ROWS : (v + 1) * ROWS, :]
+            fill_tile(tile_index, tiles_open[tile_index], bank_index)
+
+        def row_unit(tile_index, place):
+            r = row_order[place]
+            waiting.append((multiply_row(tiles_open[tile_index], r), tile_index, r))
+            bank_index = place - (ROWS - 2 * BANK_ROWS + 2)
+            if tile_index + 1 < VECTOR_TILES and 0 <= bank_index < BANK_ROWS:
+                open_step(tile_index + 1, bank_index)
+            if len(waiting) > SUM_LAG:
+                sum_oldest()
+
+        units = [
+            lambda v=v, place=place: row_unit(v, place)
+            for v in range(VECTOR_TILES)
+            for place in range(ROWS)
+        ]
+        units += [sum_oldest] * SUM_LAG
+
+        STEPS_A_BLOCK = BLOCK_T // BANK_MATMULS
+        total_steps = STEPS_A_BLOCK * BLOCKS
+        with tc.manual_schedule():
+            for bank_index in range(BANK_ROWS):
+                open_step(0, bank_index)
+            pieces = []
+            operands = {}
+            done = 0
+            for step in range(total_steps + HALF_T // BANK_MATMULS):
+                block, quarter = divmod(step, STEPS_A_BLOCK)
+                if block < BLOCKS:
+                    if quarter == 0:
+                        operands[block] = open_block(block)
+                        g = block // GROUP_BLOCKS + 1
+                        if block % GROUP_BLOCKS == 0 and g < FULL_GROUPS:
+                            pieces += full_group_pieces(g)
+                    project_step(block, operands[block], quarter)
+                if block > 0:
+                    score_step(block - 1, operands[block - 1], quarter * BANK_MATMULS)
+                if pieces:
+                    pieces.pop(0)()
+                if block > 0 and quarter == STEPS_A_BLOCK - 1 and block % GROUP_BLOCKS == 0:
+                    end = block * BLOCK_T
+                    pieces += finish_pieces(end - P, end, 0)
+                while done < len(units) and done * total_steps < (step + 1) * len(units):
+                    units[done]()
+                    done += 1
+            for piece in pieces + finish_pieces(FULL_GROUPS * P, TENSOR_T, HALF):
+                piece()

@@ -35,41 +35,41 @@ GROUPS = TOKENS // GROUP_TOKENS
 FULL_GROUPS = 3
 BLOCK_T = 32
 GROUP_BLOCKS = P // BLOCK_T
-BLOCK_TOKENS = BLOCK_T * RUNS
+SUPER_T = 2 * BLOCK_T
+SUPER_COLS = SUPER_T * RUNS
 HALF_T = 16
 LAST_T = BLOCK_T + HALF_T
 TENSOR_T = FULL_GROUPS * P + LAST_T
 BLOCKS = FULL_GROUPS * GROUP_BLOCKS + 2
+SUPERS = BLOCKS // 2
 VECTOR_T = P - LAST_T
 VECTOR_TILES = VECTOR_T * RUNS // P
 
-LAST_COL = FULL_GROUPS * GROUP_TOKENS
-HALF_COL = LAST_COL + BLOCK_TOKENS
-VECTOR_COL = HALF_COL + BLOCK_TOKENS
+VECTOR_COL = SUPERS * SUPER_COLS
 X_COLS = VECTOR_COL + VECTOR_TILES * P
+K_ROWS = BANK // (SUPER_T * PAIRS)
 
 SCORE_COLS = DIFFS * PAIRS
 BANK_MATMULS = 8
 
-PADDED = 2 * ROWS * D
-PADDED_ALL = PADDED + D
+W_COLS = ROWS * D
+PADDED = 2 * W_COLS + D
+TILE_ROWS = BANK // D
 
-VECTOR_ROWS = 2
+VECTOR_ROWS = 1
 SUM_LAG = 2
 
 FLOPS = 2 * TOKENS * C * 2 * ROWS * D + 2 * TOKENS * ROWS * ROWS * D
 
 
-def transpose_words(nc, psum, ident, rows_f32, blocks):
-    planes = psum.tile([P, 2, blocks * P], F32, tag="planes")
-    for b in range(blocks):
+def transpose_words(nc, planes, ident, rows_f32, blocks):
+    for i, b in enumerate(blocks):
         for u in range(2):
             nc.tensor.transpose(
-                planes[:, u, b * P : (b + 1) * P],
+                planes[:, u, i * P : (i + 1) * P],
                 rows_f32[:, b * WORDS + u : (b + 1) * WORDS : 2],
                 ident[:],
             )
-    return planes
 
 
 def tile_differentialattention_pa_t_kernel(tc, x, Wq, Wk, lq1, lq2, lk1, lk2, out):
@@ -82,22 +82,34 @@ def tile_differentialattention_pa_t_kernel(tc, x, Wq, Wk, lq1, lq2, lk1, lk2, ou
         tc.tile_pool(name="stage", bufs=2) as stage,
         tc.tile_pool(name="tensor_way", bufs=1) as tensor_way,
         tc.tile_pool(name="vector_way", bufs=2) as vector_way,
-        tc.tile_pool(name="products", bufs=6) as products,
+        tc.tile_pool(name="products", bufs=4) as products,
         tc.psum_pool(name="psum_t", bufs=2) as psum_t,
-        tc.psum_pool(name="psum_y", bufs=3) as psum_y,
+        tc.psum_pool(name="psum_y", bufs=4) as psum_y,
         tc.psum_pool(name="psum_s", bufs=2) as psum_s,
-        tc.psum_pool(name="psum_q", bufs=1) as psum_q,
     ):
         ident = keep.tile([P, P], F32)
         make_identity(nc, ident[:])
 
         dense_flat = keep.tile([P, TENSOR_T * DIFFS], F32, align_bytes=64)
-        dense = dense_flat[:].rearrange("p (t m) -> p t m", m=DIFFS)
-        w_grouped = []
-        for turn in range(2):
-            words = dense_flat[:, turn * PADDED : (turn + 1) * PADDED]
-            nc.gpsimd.memset(words, 0.0)
-            w_grouped.append(words)
+        dense = dense_flat[:].rearrange("p (m t) -> p m t", t=TENSOR_T)
+        w_words = {}
+        for w in range(2):
+            w_words[w] = dense_flat[:, w * 2 * W_COLS : (w + 1) * 2 * W_COLS]
+        vec_words = dense_flat[:, 4 * W_COLS : 4 * W_COLS + 2 * VECTOR_TILES * P]
+        last_first = 4 * W_COLS + 2 * VECTOR_TILES * P
+        last_words = dense_flat[:, last_first : last_first + 2 * SUPER_COLS]
+
+        w_codes = {}
+        w_scales = {}
+        w_padded = {}
+        w_padded_scales = {}
+        for w in range(2):
+            w_codes[w] = keep.tile([P, W_COLS], U32, name="codes_%d" % w, align_bytes=64)
+            w_scales[w] = keep.tile([P, W_COLS], U8, name="scales_%d" % w, align_bytes=64)
+            w_padded[w] = keep.tile([P, PADDED], U32, name="padded_%d" % w, align_bytes=64)
+            w_padded_scales[w] = keep.tile([P, PADDED], U8, name="padded_scales_%d" % w, align_bytes=64)
+            nc.gpsimd.memset(w_padded[w][:].bitcast(I32), 0)
+            nc.gpsimd.memset(w_padded_scales[w][:].bitcast(I32), 0)
 
         q_diag = []
         for turn in range(2):
@@ -111,37 +123,48 @@ def tile_differentialattention_pa_t_kernel(tc, x, Wq, Wk, lq1, lq2, lk1, lk2, ou
             else:
                 nc.vector.tensor_copy(**operands)
 
-        w_codes = {}
-        w_scales = {}
+        head_banks = [0]
+
+        def head_planes():
+            head_banks[0] += 1
+            if head_banks[0] % 3 == 0:
+                return psum_t.tile([P, 2, 2 * P], F32, name="planes", tag="planes")
+            return psum_y.tile([P, 2, 2 * P], F32, name="planes", tag="y")
+
         for w, W in ((1, Wk), (0, Wq)):
-            codes = keep.tile([P, PADDED_ALL], U32, name="codes_%d" % w, align_bytes=64)
-            scales = keep.tile([P, PADDED_ALL], U8, name="scales_%d" % w, align_bytes=64)
-            nc.vector.memset(codes[:, PADDED:].bitcast(I32), 0)
-            nc.vector.memset(scales[:, PADDED:].bitcast(I32), 0)
+            by_row = w_words[w].rearrange("p (a j d u) -> p a j d u", a=HEADS, j=2, d=D)
             for part in range(2):
-                w_sb = stage.tile([P, HEADS // 2 * C], BF16, tag="loaded", bufs=3)
+                w_sb = products.tile([P, HEADS // 2 * C], BF16, tag="prod")
                 nc.sync.dma_start(
                     out=w_sb[:].rearrange("p (a c) -> p a c", c=C),
                     in_=W[part * 512 : (part + 1) * 512, :].rearrange("(a p) c -> p a c", p=P),
                 )
                 w_f32 = w_sb[:].bitcast(F32)
-                grouped = w_grouped[part]
-                by_row = grouped.rearrange(
-                    "p (a j z d u) -> p a j z d u", a=HEADS // 2, j=2, z=2, d=D
-                )
-                for a0 in range(0, HEADS // 2, 2):
-                    planes = transpose_words(
-                        nc, psum_t, ident, w_f32[:, a0 * WORDS : (a0 + 2) * WORDS], 2
-                    )
+                for pair in range(2):
+                    a0 = part * HEADS // 2 + 2 * pair
+                    planes = head_planes()
+                    transpose_words(nc, planes, ident, w_f32, (2 * pair, 2 * pair + 1))
                     by_j = planes[:].rearrange("p u (a d j) -> p j a d u", a=2, j=2)
                     for j in range(2):
-                        copy_out(a0 // 2, out=by_row[:, a0 : a0 + 2, j, 1], in_=by_j[:, j])
-                cols = slice(part * PADDED // 2, (part + 1) * PADDED // 2)
+                        copy_out(pair, out=by_row[:, a0 : a0 + 2, j], in_=by_j[:, j])
+                cols = slice(part * W_COLS // 2, (part + 1) * W_COLS // 2)
                 nc.vector.quantize_mx(
-                    out=codes[:, cols].bitcast(FP8X4), scales=scales[:, cols], in_=grouped.bitcast(BF16)
+                    out=w_codes[w][:, cols].bitcast(FP8X4),
+                    scales=w_scales[w][:, cols],
+                    in_=w_words[w][:, part * W_COLS : (part + 1) * W_COLS].bitcast(BF16),
                 )
-            w_codes[w] = codes
-            w_scales[w] = scales
+
+        def pad_weights(w):
+            for narrow, wide, words in (
+                (w_codes[w], w_padded[w], D),
+                (w_scales[w], w_padded_scales[w], D // 4),
+            ):
+                nc.vector.tensor_copy(
+                    out=wide[:].bitcast(I32)[:, words:].rearrange(
+                        "p (r z w) -> p r z w", z=2, w=words
+                    )[:, :, 0, :],
+                    in_=narrow[:].bitcast(I32).rearrange("p (r w) -> p r w", w=words),
+                )
 
         x_codes = keep.tile([P, X_COLS], U32, align_bytes=64)
         x_scales = keep.tile([P, X_COLS], U8, align_bytes=64)
@@ -154,7 +177,7 @@ def tile_differentialattention_pa_t_kernel(tc, x, Wq, Wk, lq1, lq2, lk1, lk2, ou
 
         x_words = {}
         for g in [GROUPS - 1] + list(range(FULL_GROUPS)):
-            x_sb = stage.tile([P, RUNS * C], BF16, tag="loaded", bufs=3)
+            x_sb = stage.tile([P, RUNS * C], BF16, tag="loaded", bufs=2)
             nc.sync.dma_start(
                 out=x_sb[:],
                 in_=x_rows[g * GROUP_TOKENS : (g + 1) * GROUP_TOKENS, :].rearrange(
@@ -163,56 +186,64 @@ def tile_differentialattention_pa_t_kernel(tc, x, Wq, Wk, lq1, lq2, lk1, lk2, ou
             )
             x_words[g] = x_sb[:].bitcast(F32)
 
+        def super_view(words):
+            return words.rearrange(
+                "p (b s t h n u) -> p b s h t n u", s=2, t=SUPER_T, h=2, n=2, u=2
+            )
+
+        def turn_runs(words, planes, s, h):
+            first = 4 * h + s
+            transpose_words(nc, planes, ident, words, (first, first + 2))
+
         def prepare_last_group():
-            last = stage.tile([P, 4 * 2 * BLOCK_TOKENS], BF16, tag="grouped", align_bytes=64)
-            last_words = last[:].bitcast(F32)
-            by_half = last_words[:, : 2 * BLOCK_TOKENS].rearrange(
-                "p (s n t u) -> p s n t u", s=2, n=PAIRS, u=2
-            )
-            short = last_words[:, 2 * BLOCK_TOKENS :].rearrange(
-                "p (i s n t u) -> p i s n t u", i=2, s=2, n=PAIRS, u=2
-            )
-            vec = stage.tile([P, 4 * VECTOR_TILES * P], BF16, tag="vec", bufs=1, align_bytes=64)
-            by_run = vec[:].bitcast(F32).rearrange("p (y t u) -> p y t u", y=RUNS, u=2)
-            for n in range(PAIRS):
-                planes = transpose_words(
-                    nc, psum_t, ident, x_words[GROUPS - 1][:, 2 * n * WORDS : (2 * n + 2) * WORDS], 2
-                )
-                by_time = planes[:].rearrange("p u (s t) -> p s t u", s=2)
-                copy_out(n, out=by_run[:, 2 * n : 2 * n + 2], in_=by_time[:, :, LAST_T:, :])
-                copy_out(n, out=by_half[:, :, n], in_=by_time[:, :, :BLOCK_T, :])
-                for i in range(2):
-                    copy_out(n, out=short[:, i, :, n], in_=by_time[:, :, BLOCK_T:LAST_T, :])
-            for first, tiles in ((0, 2), (2, 2), (4, 1)):
-                quantise_x(VECTOR_COL + first * P, vec[:, 4 * first * P : 4 * (first + tiles) * P])
-            quantise_x(LAST_COL, last[:])
-
-        def full_group_pieces(g):
-            grouped = stage.tile([P, 4 * GROUP_TOKENS], BF16, tag="grouped", align_bytes=64)
-            by_block = grouped[:].bitcast(F32).rearrange(
-                "p (b s n t u) -> p b s n t u", b=GROUP_BLOCKS, s=2, n=PAIRS, u=2
-            )
-
-            def turn_pair(n):
-                planes = transpose_words(
-                    nc, psum_t, ident, x_words[g][:, 2 * n * WORDS : (2 * n + 2) * WORDS], 2
-                )
+            by_super = super_view(last_words)
+            by_run = vec_words.rearrange("p (y t u) -> p y t u", y=RUNS, u=2)
+            for h in range(2):
                 for s in range(2):
-                    copy_out(
-                        n,
-                        out=by_block[:, :, s, n],
-                        in_=planes[:, :, s * P : (s + 1) * P].rearrange(
-                            "p u (b t) -> p b t u", b=GROUP_BLOCKS
-                        ),
+                    planes = head_planes()
+                    turn_runs(x_words[GROUPS - 1], planes, s, h)
+                    by_time = planes[:].rearrange("p u (n t) -> p n t u", n=2)
+                    first = 4 * h + s
+                    nc.scalar.copy(
+                        out=by_run[:, first : first + 3 : 2], in_=by_time[:, :, LAST_T:, :]
+                    )
+                    nc.scalar.copy(
+                        out=by_super[:, 0, s, h],
+                        in_=planes[:].rearrange("p u (n t) -> p t n u", n=2)[:, :SUPER_T],
+                    )
+            for first, tiles in ((0, 2), (2, 2), (4, 1)):
+                quantise_x(
+                    VECTOR_COL + first * P,
+                    vec_words[:, 2 * first * P : 2 * (first + tiles) * P].bitcast(BF16),
+                )
+            quantise_x(FULL_GROUPS * GROUP_TOKENS, last_words.bitcast(BF16))
+
+        def full_group_pieces(g, new_planes):
+            grouped = stage.tile([P, 4 * GROUP_TOKENS], BF16, tag="grouped", bufs=1, align_bytes=64)
+            by_super = super_view(grouped[:].bitcast(F32))
+
+            def turn(s, h):
+                planes = new_planes()
+                turn_runs(x_words[g], planes, s, h)
+                for b in range(2):
+                    nc.scalar.copy(
+                        out=by_super[:, b, s, h],
+                        in_=planes[:].rearrange("p u (n b t) -> p b t n u", n=2, b=2)[:, b],
                     )
 
-            pieces = [lambda n=n: turn_pair(n) for n in range(PAIRS)]
+            pieces = [lambda s=s, h=h: turn(s, h) for s in range(2) for h in range(2)]
             pieces.append(lambda: quantise_x(g * GROUP_TOKENS, grouped[:]))
             return pieces
 
         prepare_last_group()
-        for piece in full_group_pieces(0):
+        for w in (1, 0):
+            pad_weights(w)
+        for piece in full_group_pieces(0, head_planes):
             piece()
+
+        def loop_planes():
+            return psum_t.tile([P, 2, 2 * P], F32, name="planes", tag="planes")
+
 
         vectors = keep.tile([P, 4, D], BF16)
         for v, vector in enumerate((lq1, lq2, lk1, lk2)):
@@ -233,69 +264,70 @@ def tile_differentialattention_pa_t_kernel(tc, x, Wq, Wk, lq1, lq2, lk1, lk2, ou
 
         neg_max = keep.tile([P, TENSOR_T], F32)
 
-        def project_pairs(w, bank_index, first_cols):
-            bank = psum_y.tile([P, BANK_ROWS, P], F32, tag="y")
-            for i in range(BANK_ROWS):
-                r = bank_index * BANK_ROWS + i
-                for s in range(2):
-                    w_cols = slice(P * r + D * (1 - s), P * r + D * (1 - s) + P)
-                    x_cols = slice(first_cols[s], first_cols[s] + P)
-                    nc.tensor.matmul_mx(
-                        out=bank[:, i, :],
-                        lhsT=w_codes[w][:, w_cols].bitcast(FP8X4),
-                        lhsT_scale=w_scales[w][:, w_cols],
-                        rhs=x_codes[:, x_cols].bitcast(FP8X4),
-                        rhs_scale=x_scales[:, x_cols],
-                        start=(s == 0),
-                        stop=(s == 1),
-                    )
-            return bank
+        def project_pairs(bank, w, r, first, cols):
+            for s in range(2):
+                w_cols = slice(P * r + D * (1 - s), P * r + D * (1 - s) + P)
+                x_cols = slice(first + s * SUPER_COLS // 2, first + s * SUPER_COLS // 2 + cols)
+                nc.tensor.matmul_mx(
+                    out=bank,
+                    lhsT=w_padded[w][:, w_cols].bitcast(FP8X4),
+                    lhsT_scale=w_padded_scales[w][:, w_cols],
+                    rhs=x_codes[:, x_cols].bitcast(FP8X4),
+                    rhs_scale=x_scales[:, x_cols],
+                    start=(s == 0),
+                    stop=(s == 1),
+                )
 
         def block_times(block):
             return BLOCK_T if block < BLOCKS - 1 else HALF_T
 
-        def open_block(block):
-            k_pairs = tensor_way.tile([P, BLOCK_T, DIFFS, PAIRS], F32, bufs=2)
-            k_first = tensor_way.tile([P, BLOCK_T, PAIRS], F32, bufs=2)
-            return q_diag[block % 2], k_pairs, k_first
+        def open_super(index):
+            k_pairs = tensor_way.tile([P, SUPER_T, DIFFS, PAIRS], F32, bufs=2)
+            k_first = tensor_way.tile([P, SUPER_T, PAIRS], F32)
+            return k_pairs, k_first
 
-        def project_step(block, operands, bank_index):
-            diag, k_pairs, k_first = operands
-            times = block_times(block)
-            if block < BLOCKS - 1:
-                first_cols = (block * BLOCK_TOKENS, block * BLOCK_TOKENS + P)
-            else:
-                first_cols = (HALF_COL, HALF_COL + HALF)
-            rows = slice(bank_index * BANK_ROWS, (bank_index + 1) * BANK_ROWS)
-            bank = project_pairs(1, bank_index, first_cols)
-            by_time = bank[:, :, : PAIRS * times].rearrange("p i (n t) -> p t i n", n=PAIRS)
+        def k_step(index, operands, bank_index):
+            k_pairs, k_first = operands
+            times = SUPER_T if index < SUPERS - 1 else LAST_T
+            bank = psum_y.tile([P, K_ROWS, SUPER_T * PAIRS], F32, tag="y")
+            for i in range(K_ROWS):
+                r = bank_index * K_ROWS + i
+                project_pairs(bank[:, i, :], 1, r, index * SUPER_COLS, SUPER_T * PAIRS)
+            by_time = bank[:].rearrange("p i (t n) -> p t i n", n=PAIRS)[:, :times]
             skip = 1 if bank_index == 0 else 0
             if skip:
                 nc.scalar.copy(out=k_first[:, :times], in_=by_time[:, :, 0])
-            first = bank_index * BANK_ROWS + skip - 1
-            count = BANK_ROWS - skip
+            first = bank_index * K_ROWS + skip - 1
+            count = K_ROWS - skip
             nc.vector.tensor_tensor(
                 out=k_pairs[:, :times, first : first + count, :],
                 in0=by_time[:, :, skip:],
                 in1=k_first[:, :times].unsqueeze(2).to_broadcast([P, times, count, PAIRS]),
                 op=ALU.subtract,
             )
-            bank = project_pairs(0, bank_index, first_cols)
+
+        def q_step(block, diag, bank_index):
+            cols = block_times(block) * PAIRS
+            first = block // 2 * SUPER_COLS + block % 2 * BLOCK_T * PAIRS
+            bank = psum_y.tile([P, BANK_ROWS, P], F32, tag="y")
+            for i in range(BANK_ROWS):
+                project_pairs(bank[:, i, :], 0, bank_index * BANK_ROWS + i, first, P)
+            rows = slice(bank_index * BANK_ROWS, (bank_index + 1) * BANK_ROWS)
+            by_token = diag[:].rearrange("p t n s r -> p s (t n) r")
             for s in range(2):
                 half = slice(s * HALF, (s + 1) * HALF)
                 nc.scalar.copy(
-                    out=diag[half, :times, :, s, rows],
-                    in_=bank[half, :, : PAIRS * times].rearrange("p i (n t) -> p t n i", n=PAIRS),
+                    out=by_token[half, s, :cols, rows],
+                    in_=bank[half, :, :cols].rearrange("p i c -> p c i"),
                 )
 
-        def score_step(block, operands, t0):
-            diag, k_pairs, k_first = operands
+        def score_step(block, diag, k_pairs, t0):
             raw = psum_s.tile([P, BANK_MATMULS, SCORE_COLS], F32, tag="raw")
             for i in range(BANK_MATMULS):
                 nc.tensor.matmul(
                     out=raw[:, i, :],
                     lhsT=diag[:, t0 + i].rearrange("p n s r -> p (n s r)"),
-                    rhs=k_pairs[:, t0 + i].rearrange("p m n -> p (m n)"),
+                    rhs=k_pairs[:, block % 2 * BLOCK_T + t0 + i].rearrange("p m n -> p (m n)"),
                     start=True,
                     stop=True,
                 )
@@ -303,23 +335,27 @@ def tile_differentialattention_pa_t_kernel(tc, x, Wq, Wk, lq1, lq2, lk1, lk2, ou
             for n in range(PAIRS):
                 quad = slice(n * QUADRANT, (n + 1) * QUADRANT)
                 nc.scalar.copy(
-                    out=dense[quad, first : first + BANK_MATMULS, :],
-                    in_=raw[quad].rearrange("p i (m n) -> p i m n", n=PAIRS)[:, :, :, n],
+                    out=dense[quad, :, first : first + BANK_MATMULS],
+                    in_=raw[quad].rearrange("p i (m n) -> p m i n", n=PAIRS)[:, :, :, n],
                 )
+
+        def find_max(block):
+            first = block * BLOCK_T
+            new = slice(first, first + block_times(block))
+            nc.vector.tensor_reduce(
+                out=neg_max[:, new],
+                in_=dense[:, :, new].rearrange("p m t -> p t m"),
+                axis=AXIS_X,
+                op=ALU.max,
+            )
+            nc.vector.tensor_scalar(
+                out=neg_max[:, new], in0=neg_max[:, new], scalar1=-1.0, scalar2=0.0,
+                op0=ALU.mult, op1=ALU.min,
+            )
 
         def finish_pieces(first_new, end, lo):
-            new = slice(first_new, end)
             first = end - P
-            exps = tensor_way.tile([P, P, ROWS], F32)
-
-            def find_max():
-                nc.vector.tensor_reduce(
-                    out=neg_max[:, new], in_=dense[:, new, :], axis=AXIS_X, op=ALU.max
-                )
-                nc.vector.tensor_scalar(
-                    out=neg_max[:, new], in0=neg_max[:, new], scalar1=-1.0, scalar2=0.0,
-                    op0=ALU.mult, op1=ALU.min,
-                )
+            exps = tensor_way.tile([P, P, ROWS], F32, bufs=2)
 
             def turn_and_exp(m0):
                 flipped = psum_t.tile([P, BANK_ROWS, P], F32, tag="planes")
@@ -328,7 +364,7 @@ def tile_differentialattention_pa_t_kernel(tc, x, Wq, Wk, lq1, lq2, lk1, lk2, ou
                     if m > 0:
                         nc.tensor.matmul(
                             out=flipped[:, i, :],
-                            lhsT=dense[:, first:end, m - 1],
+                            lhsT=dense[:, m - 1, first:end],
                             rhs=ident[:],
                             start=True,
                             stop=False,
@@ -383,15 +419,14 @@ def tile_differentialattention_pa_t_kernel(tc, x, Wq, Wk, lq1, lq2, lk1, lk2, ou
                     in_=result[first_new - first :].rearrange("p e h -> p (e h)"),
                 )
 
-            pieces = [find_max]
-            pieces += [lambda m0=m0: turn_and_exp(m0) for m0 in range(0, ROWS, BANK_ROWS)]
+            pieces = [lambda m0=m0: turn_and_exp(m0) for m0 in range(0, ROWS, BANK_ROWS)]
             pieces += [find_factors, combine]
             return pieces
 
-        def project_tile(w, bank_index, tile_index, pool, tag):
-            bank = pool.tile([P, BANK], F32, tag=tag)
+        def project_tile(w, bank_index, tile_index):
+            bank = psum_y.tile([P, BANK], F32, tag="y")
             tok = slice(VECTOR_COL + tile_index * P, VECTOR_COL + (tile_index + 1) * P)
-            w_cols = slice(D + bank_index * BANK, D + (bank_index + 1) * BANK)
+            w_cols = slice(bank_index * BANK, (bank_index + 1) * BANK)
             nc.tensor.matmul_mx(
                 out=bank[:],
                 lhsT=x_codes[:, tok].bitcast(FP8X4),
@@ -401,43 +436,46 @@ def tile_differentialattention_pa_t_kernel(tc, x, Wq, Wk, lq1, lq2, lk1, lk2, ou
                 start=True,
                 stop=True,
             )
-            return bank[:].rearrange("p (i z d) -> p i z d", z=2, d=D)[:, :, 0, :]
+            return bank[:].rearrange("p (i d) -> p i d", d=D)
 
         def open_tile(tile_index):
-            q_psum = project_tile(0, 0, tile_index, psum_q, "q")
             q_sb = vector_way.tile([P, ROWS, D], F32)
             k_sb = vector_way.tile([P, DIFFS, D], F32)
-            k_zero = vector_way.tile([P, D], F32)
-            return q_psum, q_sb, k_sb, k_zero
+            return q_sb, k_sb
 
-        def fill_tile(tile_index, operands, bank_index):
-            q_psum, q_sb, k_sb, k_zero = operands
-            bank = project_tile(1, bank_index, tile_index, psum_y, "y")
-            skip = 1 if bank_index == 0 else 0
-            if skip:
-                nc.scalar.copy(out=k_zero[:], in_=bank[:, 0])
-            first = bank_index * BANK_ROWS + skip - 1
-            count = BANK_ROWS - skip
-            nc.vector.tensor_tensor(
-                out=k_sb[:, first : first + count, :],
-                in0=bank[:, skip:],
-                in1=k_zero[:].unsqueeze(1).to_broadcast([P, count, D]),
-                op=ALU.subtract,
-            )
-            if bank_index == 0:
-                nc.scalar.copy(out=q_sb[:, VECTOR_ROWS:BANK_ROWS, :], in_=q_psum[:, VECTOR_ROWS:])
-            else:
-                nc.scalar.copy(
-                    out=q_sb[:, bank_index * BANK_ROWS : (bank_index + 1) * BANK_ROWS, :],
-                    in_=project_tile(0, bank_index, tile_index, psum_y, "y"),
+        def fill_k(tile_index, operands):
+            q_sb, k_sb = operands
+            k_zero = vector_way.tile([P, D], F32)
+            for bank_index in range(ROWS // TILE_ROWS):
+                bank = project_tile(1, bank_index, tile_index)
+                skip = 1 if bank_index == 0 else 0
+                if skip:
+                    nc.scalar.copy(out=k_zero[:], in_=bank[:, 0])
+                first = bank_index * TILE_ROWS + skip - 1
+                count = TILE_ROWS - skip
+                nc.vector.tensor_tensor(
+                    out=k_sb[:, first : first + count, :],
+                    in0=bank[:, skip:],
+                    in1=k_zero[:].unsqueeze(1).to_broadcast([P, count, D]),
+                    op=ALU.subtract,
                 )
 
-        def multiply_row(operands, r):
-            q_psum, q_sb, k_sb, k_zero = operands
-            prod = products.tile([P, DIFFS, D], F32)
-            on_vector = r < VECTOR_ROWS
-            engine = nc.vector if on_vector else nc.gpsimd
-            q_row = q_psum[:, r, :] if on_vector else q_sb[:, r, :]
+        def fill_q(tile_index, operands):
+            q_sb, k_sb = operands
+            made = []
+            for bank_index in range(ROWS // TILE_ROWS):
+                bank = project_tile(0, bank_index, tile_index)
+                skip = VECTOR_ROWS if bank_index == 0 else 0
+                nc.scalar.copy(
+                    out=q_sb[:, bank_index * TILE_ROWS + skip : (bank_index + 1) * TILE_ROWS, :],
+                    in_=bank[:, skip:],
+                )
+                for r in range(skip):
+                    made.append(multiply_row(nc.vector, bank[:, r, :], k_sb))
+            return made
+
+        def multiply_row(engine, q_row, k_sb):
+            prod = products.tile([P, DIFFS, D], F32, tag="prod")
             engine.tensor_tensor(
                 out=prod[:],
                 in0=q_row.unsqueeze(1).to_broadcast([P, DIFFS, D]),
@@ -493,7 +531,6 @@ def tile_differentialattention_pa_t_kernel(tc, x, Wq, Wk, lq1, lq2, lk1, lk2, ou
                     p0 += count
 
         BATCHES = ((0, 3), (3, 2))
-        row_order = [2, 3, 0] + list(range(4, 8)) + [1] + list(range(8, ROWS))
         tiles_open = {}
         scores_of = {}
         waiting = []
@@ -503,65 +540,91 @@ def tile_differentialattention_pa_t_kernel(tc, x, Wq, Wk, lq1, lq2, lk1, lk2, ou
             nc.vector.tensor_reduce(
                 out=scores_of[tile_index][:, r, 1:], in_=prod[:], axis=AXIS_X, op=ALU.add
             )
-            if r == row_order[-1]:
+            if r == ROWS - 1:
                 for first_tile, tiles in BATCHES:
                     if tile_index == first_tile + tiles - 1:
                         finish_batch(first_tile, tiles, scores_of["batch", first_tile])
 
-        def open_step(tile_index, bank_index):
-            if bank_index == 0:
-                tiles_open[tile_index] = open_tile(tile_index)
-                for first_tile, tiles in BATCHES:
-                    if tile_index == first_tile:
-                        batch = vector_way.tile([P, tiles * ROWS, ROWS], F32)
-                        nc.vector.memset(batch[:, :, 0:1], 0.0)
-                        scores_of["batch", first_tile] = batch
-                        for v in range(tiles):
-                            scores_of[first_tile + v] = batch[:, v * ROWS : (v + 1) * ROWS, :]
-            fill_tile(tile_index, tiles_open[tile_index], bank_index)
+        def open_k(tile_index):
+            tiles_open[tile_index] = open_tile(tile_index)
+            for first_tile, tiles in BATCHES:
+                if tile_index == first_tile:
+                    batch = vector_way.tile([P, tiles * ROWS, ROWS], F32)
+                    nc.vector.memset(batch[:, :, 0:1], 0.0)
+                    scores_of["batch", first_tile] = batch
+                    for v in range(tiles):
+                        scores_of[first_tile + v] = batch[:, v * ROWS : (v + 1) * ROWS, :]
+            fill_k(tile_index, tiles_open[tile_index])
 
-        def row_unit(tile_index, place):
-            r = row_order[place]
-            waiting.append((multiply_row(tiles_open[tile_index], r), tile_index, r))
-            bank_index = place - (ROWS - 2 * BANK_ROWS + 2)
-            if tile_index + 1 < VECTOR_TILES and 0 <= bank_index < BANK_ROWS:
-                open_step(tile_index + 1, bank_index)
-            if len(waiting) > SUM_LAG:
+        def open_q(tile_index):
+            for r, prod in enumerate(fill_q(tile_index, tiles_open[tile_index])):
+                waiting.append((prod, tile_index, r))
+
+        def row_unit(tile_index, r):
+            q_sb, k_sb = tiles_open[tile_index]
+            waiting.append((multiply_row(nc.gpsimd, q_sb[:, r, :], k_sb), tile_index, r))
+            if tile_index + 1 < VECTOR_TILES and r == ROWS - 5:
+                open_k(tile_index + 1)
+            if tile_index + 1 < VECTOR_TILES and r == ROWS - 4:
+                open_q(tile_index + 1)
+            while len(waiting) > SUM_LAG:
                 sum_oldest()
 
         units = [
-            lambda v=v, place=place: row_unit(v, place)
+            lambda v=v, r=r: row_unit(v, r)
             for v in range(VECTOR_TILES)
-            for place in range(ROWS)
+            for r in range(VECTOR_ROWS, ROWS)
         ]
         units += [sum_oldest] * SUM_LAG
 
-        STEPS_A_BLOCK = BLOCK_T // BANK_MATMULS
-        total_steps = STEPS_A_BLOCK * BLOCKS
+        LEAD = 2
+        total_turns = 2 * BLOCKS
+        supers = {}
+
+        def k_turn(turn):
+            index, quarter = divmod(turn, 4)
+            if index < SUPERS:
+                if quarter == 0:
+                    supers[index] = open_super(index)
+                for i in range(2):
+                    k_step(index, supers[index], 2 * quarter + i)
+
         with tc.manual_schedule():
-            for bank_index in range(BANK_ROWS):
-                open_step(0, bank_index)
+            open_k(0)
+            open_q(0)
+            for turn in range(LEAD):
+                k_turn(turn)
             pieces = []
-            operands = {}
             done = 0
-            for step in range(total_steps + HALF_T // BANK_MATMULS):
-                block, quarter = divmod(step, STEPS_A_BLOCK)
+            for turn in range(total_turns + 1):
+                block, half = divmod(turn, 2)
+                k_turn(turn + LEAD)
                 if block < BLOCKS:
-                    if quarter == 0:
-                        operands[block] = open_block(block)
-                        g = block // GROUP_BLOCKS + 1
-                        if block % GROUP_BLOCKS == 0 and g < FULL_GROUPS:
-                            pieces += full_group_pieces(g)
-                    project_step(block, operands[block], quarter)
-                if block > 0:
-                    score_step(block - 1, operands[block - 1], quarter * BANK_MATMULS)
-                if pieces:
-                    pieces.pop(0)()
-                if block > 0 and quarter == STEPS_A_BLOCK - 1 and block % GROUP_BLOCKS == 0:
-                    end = block * BLOCK_T
-                    pieces += finish_pieces(end - P, end, 0)
-                while done < len(units) and done * total_steps < (step + 1) * len(units):
+                    for i in range(2):
+                        q_step(block, q_diag[block % 2], 2 * half + i)
+                    g = block // GROUP_BLOCKS + 1
+                    if half == 0 and block % GROUP_BLOCKS == 0 and g < FULL_GROUPS:
+                        pieces += full_group_pieces(g, loop_planes)
+                if block > 1 and half == 0:
+                    find_max(block - 2)
+                while done < len(units) and done * total_turns < (turn + 1) * len(units):
                     units[done]()
                     done += 1
+                before = block - 1
+                if block > 0:
+                    for i in range(2):
+                        score_step(
+                            before,
+                            q_diag[before % 2],
+                            supers[before // 2][0],
+                            (2 * half + i) * BANK_MATMULS,
+                        )
+                for piece in pieces[:2]:
+                    piece()
+                pieces = pieces[2:]
+                if block > 0 and half == 1 and block % GROUP_BLOCKS == 0:
+                    end = block * BLOCK_T
+                    pieces += finish_pieces(end - P, end, 0)
+            find_max(BLOCKS - 1)
             for piece in pieces + finish_pieces(FULL_GROUPS * P, TENSOR_T, HALF):
                 piece()

@@ -86,11 +86,12 @@ def tile_differentialattention_pa_t_kernel(tc, x, Wq, Wk, lq1, lq2, lk1, lk2, ou
         tc.psum_pool(name="psum_t", bufs=2) as psum_t,
         tc.psum_pool(name="psum_y", bufs=4) as psum_y,
         tc.psum_pool(name="psum_s", bufs=2) as psum_s,
+        tc.manual_schedule(),
     ):
         ident = keep.tile([P, P], F32)
         make_identity(nc, ident[:])
 
-        dense_flat = keep.tile([P, TENSOR_T * DIFFS], F32, align_bytes=64)
+        dense_flat = keep.tile([P, TENSOR_T * ROWS], F32, align_bytes=64)
         dense = dense_flat[:].rearrange("p (m t) -> p m t", t=TENSOR_T)
         w_words = {}
         for w in range(2):
@@ -98,6 +99,8 @@ def tile_differentialattention_pa_t_kernel(tc, x, Wq, Wk, lq1, lq2, lk1, lk2, ou
         vec_words = dense_flat[:, 4 * W_COLS : 4 * W_COLS + 2 * VECTOR_TILES * P]
         last_first = 4 * W_COLS + 2 * VECTOR_TILES * P
         last_words = dense_flat[:, last_first : last_first + 2 * SUPER_COLS]
+
+        nc.vector.memset(dense[:, DIFFS:], 0.0)
 
         w_codes = {}
         w_scales = {}
@@ -114,7 +117,7 @@ def tile_differentialattention_pa_t_kernel(tc, x, Wq, Wk, lq1, lq2, lk1, lk2, ou
         q_diag = []
         for turn in range(2):
             diag = keep.tile([P, BLOCK_T, PAIRS, 2, ROWS], F32, name="q_diag%d" % turn)
-            nc.gpsimd.memset(diag[:], 0.0)
+            nc.vector.memset(diag[:], 0.0)
             q_diag.append(diag)
 
         def copy_out(index, **operands):
@@ -175,8 +178,12 @@ def tile_differentialattention_pa_t_kernel(tc, x, Wq, Wk, lq1, lq2, lk1, lk2, ou
                 out=x_codes[:, cols].bitcast(FP8X4), scales=x_scales[:, cols], in_=grouped
             )
 
+        vectors = keep.tile([P, 4, D], BF16)
         x_words = {}
         for g in [GROUPS - 1] + list(range(FULL_GROUPS)):
+            if g == 1:
+                for v, vector in enumerate((lq1, lq2, lk1, lk2)):
+                    nc.sync.dma_start(out=vectors[:, v, :], in_=vector.partition_broadcast(P))
             x_sb = stage.tile([P, RUNS * C], BF16, tag="loaded", bufs=2)
             nc.sync.dma_start(
                 out=x_sb[:],
@@ -207,16 +214,16 @@ def tile_differentialattention_pa_t_kernel(tc, x, Wq, Wk, lq1, lq2, lk1, lk2, ou
                     nc.scalar.copy(
                         out=by_run[:, first : first + 3 : 2], in_=by_time[:, :, LAST_T:, :]
                     )
-                    nc.scalar.copy(
+                    nc.vector.tensor_copy(
                         out=by_super[:, 0, s, h],
                         in_=planes[:].rearrange("p u (n t) -> p t n u", n=2)[:, :SUPER_T],
                     )
-            for first, tiles in ((0, 2), (2, 2), (4, 1)):
-                quantise_x(
-                    VECTOR_COL + first * P,
-                    vec_words[:, 2 * first * P : 2 * (first + tiles) * P].bitcast(BF16),
-                )
-            quantise_x(FULL_GROUPS * GROUP_TOKENS, last_words.bitcast(BF16))
+
+        def quantise_tiles(first, tiles):
+            quantise_x(
+                VECTOR_COL + first * P,
+                vec_words[:, 2 * first * P : 2 * (first + tiles) * P].bitcast(BF16),
+            )
 
         def full_group_pieces(g, new_planes):
             grouped = stage.tile([P, 4 * GROUP_TOKENS], BF16, tag="grouped", bufs=1, align_bytes=64)
@@ -235,32 +242,24 @@ def tile_differentialattention_pa_t_kernel(tc, x, Wq, Wk, lq1, lq2, lk1, lk2, ou
             pieces.append(lambda: quantise_x(g * GROUP_TOKENS, grouped[:]))
             return pieces
 
-        prepare_last_group()
-        for w in (1, 0):
-            pad_weights(w)
-        for piece in full_group_pieces(0, head_planes):
-            piece()
-
         def loop_planes():
             return psum_t.tile([P, 2, 2 * P], F32, name="planes", tag="planes")
 
-
-        vectors = keep.tile([P, 4, D], BF16)
-        for v, vector in enumerate((lq1, lq2, lk1, lk2)):
-            nc.sync.dma_start(out=vectors[:, v, :], in_=vector.partition_broadcast(P))
         lam_products = keep.tile([P, 2, D], F32)
-        nc.vector.tensor_tensor(
-            out=lam_products[:], in0=vectors[:, 0:2, :], in1=vectors[:, 2:4, :], op=ALU.mult
-        )
         lam_dots = keep.tile([P, 2], F32)
-        nc.vector.tensor_reduce(out=lam_dots[:], in_=lam_products[:], axis=AXIS_X, op=ALU.add)
         lam_exps = keep.tile([P, 2], F32)
-        nc.scalar.activation(out=lam_exps[:], in_=lam_dots[:], func=ACT.Exp)
         neg_lam = keep.tile([P, 1], F32)
-        nc.vector.tensor_tensor(
-            out=neg_lam[:], in0=lam_exps[:, 1:2], in1=lam_exps[:, 0:1], op=ALU.subtract
-        )
-        nc.vector.tensor_scalar_add(out=neg_lam[:], in0=neg_lam[:], scalar1=-LAM_INIT)
+
+        def find_lam():
+            nc.vector.tensor_tensor(
+                out=lam_products[:], in0=vectors[:, 0:2, :], in1=vectors[:, 2:4, :], op=ALU.mult
+            )
+            nc.vector.tensor_reduce(out=lam_dots[:], in_=lam_products[:], axis=AXIS_X, op=ALU.add)
+            nc.scalar.activation(out=lam_exps[:], in_=lam_dots[:], func=ACT.Exp)
+            nc.vector.tensor_tensor(
+                out=neg_lam[:], in0=lam_exps[:, 1:2], in1=lam_exps[:, 0:1], op=ALU.subtract
+            )
+            nc.vector.tensor_scalar_add(out=neg_lam[:], in0=neg_lam[:], scalar1=-LAM_INIT)
 
         neg_max = keep.tile([P, TENSOR_T], F32)
 
@@ -335,7 +334,7 @@ def tile_differentialattention_pa_t_kernel(tc, x, Wq, Wk, lq1, lq2, lk1, lk2, ou
             for n in range(PAIRS):
                 quad = slice(n * QUADRANT, (n + 1) * QUADRANT)
                 nc.scalar.copy(
-                    out=dense[quad, :, first : first + BANK_MATMULS],
+                    out=dense[quad, :DIFFS, first : first + BANK_MATMULS],
                     in_=raw[quad].rearrange("p i (m n) -> p m i n", n=PAIRS)[:, :, :, n],
                 )
 
@@ -347,10 +346,7 @@ def tile_differentialattention_pa_t_kernel(tc, x, Wq, Wk, lq1, lq2, lk1, lk2, ou
                 in_=dense[:, :, new].rearrange("p m t -> p t m"),
                 axis=AXIS_X,
                 op=ALU.max,
-            )
-            nc.vector.tensor_scalar(
-                out=neg_max[:, new], in0=neg_max[:, new], scalar1=-1.0, scalar2=0.0,
-                op0=ALU.mult, op1=ALU.min,
+                negate=True,
             )
 
         def finish_pieces(first_new, end, lo):
@@ -392,25 +388,28 @@ def tile_differentialattention_pa_t_kernel(tc, x, Wq, Wk, lq1, lq2, lk1, lk2, ou
                 row_sum = tensor_way.tile([P, P], F32, bufs=2)
                 nc.vector.tensor_reduce(out=row_sum[lo:], in_=exps[lo:], axis=AXIS_X, op=ALU.add)
                 nc.vector.reciprocal(out=factor[lo:], in_=row_sum[lo:])
-                nc.vector.tensor_scalar_mul(
-                    out=by_j[lo:, 1], in0=by_j[lo:, 1], scalar1=neg_lam[lo:, 0:1]
-                )
 
             def combine():
                 by_parity = exps[:].rearrange("p (e j) (h i) -> p j i e h", j=2, i=2)
-                terms = []
-                for j in range(2):
-                    term = tensor_way.tile([P, RUNS * HEADS, HEADS], F32, name="term%d" % j)
-                    nc.vector.tensor_tensor(
-                        out=term[lo:],
-                        in0=by_parity[lo:, j, j],
-                        in1=by_j[lo:, j].unsqueeze(2).to_broadcast([P - lo, RUNS * HEADS, HEADS]),
-                        op=ALU.mult,
-                    )
-                    terms.append(term)
+                shape = [P - lo, RUNS * HEADS, HEADS]
                 result = tensor_way.tile([P, RUNS * HEADS, HEADS], F32)
+                odd_part = tensor_way.tile([P, RUNS * HEADS, HEADS], F32)
+                nc.vector.scalar_tensor_tensor(
+                    out=odd_part[lo:],
+                    in0=by_parity[lo:, 1, 1],
+                    scalar=neg_lam[lo:, 0:1],
+                    in1=by_j[lo:, 1].unsqueeze(2).to_broadcast(shape),
+                    op0=ALU.mult,
+                    op1=ALU.mult,
+                )
                 nc.vector.tensor_tensor(
-                    out=result[lo:], in0=terms[0][lo:], in1=terms[1][lo:], op=ALU.add
+                    out=result[lo:],
+                    in0=by_parity[lo:, 0, 0],
+                    in1=by_j[lo:, 0].unsqueeze(2).to_broadcast(shape),
+                    op=ALU.mult,
+                )
+                nc.vector.tensor_tensor(
+                    out=result[lo:], in0=result[lo:], in1=odd_part[lo:], op=ALU.add
                 )
                 nc.sync.dma_start(
                     out=out_rows[first_new * RUNS : end * RUNS, :].rearrange(
@@ -589,42 +588,51 @@ def tile_differentialattention_pa_t_kernel(tc, x, Wq, Wk, lq1, lq2, lk1, lk2, ou
                 for i in range(2):
                     k_step(index, supers[index], 2 * quarter + i)
 
-        with tc.manual_schedule():
-            open_k(0)
-            open_q(0)
-            for turn in range(LEAD):
-                k_turn(turn)
-            pieces = []
-            done = 0
-            for turn in range(total_turns + 1):
-                block, half = divmod(turn, 2)
-                k_turn(turn + LEAD)
-                if block < BLOCKS:
-                    for i in range(2):
-                        q_step(block, q_diag[block % 2], 2 * half + i)
-                    g = block // GROUP_BLOCKS + 1
-                    if half == 0 and block % GROUP_BLOCKS == 0 and g < FULL_GROUPS:
-                        pieces += full_group_pieces(g, loop_planes)
-                if block > 1 and half == 0:
-                    find_max(block - 2)
-                while done < len(units) and done * total_turns < (turn + 1) * len(units):
-                    units[done]()
-                    done += 1
-                before = block - 1
-                if block > 0:
-                    for i in range(2):
-                        score_step(
-                            before,
-                            q_diag[before % 2],
-                            supers[before // 2][0],
-                            (2 * half + i) * BANK_MATMULS,
-                        )
-                for piece in pieces[:2]:
-                    piece()
-                pieces = pieces[2:]
-                if block > 0 and half == 1 and block % GROUP_BLOCKS == 0:
-                    end = block * BLOCK_T
-                    pieces += finish_pieces(end - P, end, 0)
-            find_max(BLOCKS - 1)
-            for piece in pieces + finish_pieces(FULL_GROUPS * P, TENSOR_T, HALF):
+        prepare_last_group()
+        quantise_tiles(0, 2)
+        open_k(0)
+        open_q(0)
+        for piece in full_group_pieces(0, head_planes):
+            piece()
+        for w in (1, 0):
+            pad_weights(w)
+        for turn in range(LEAD):
+            k_turn(turn)
+        quantise_tiles(2, 2)
+        quantise_tiles(4, 1)
+        quantise_x(FULL_GROUPS * GROUP_TOKENS, last_words.bitcast(BF16))
+        find_lam()
+        pieces = []
+        done = 0
+        for turn in range(total_turns + 1):
+            block, half = divmod(turn, 2)
+            k_turn(turn + LEAD)
+            if block < BLOCKS:
+                for i in range(2):
+                    q_step(block, q_diag[block % 2], 2 * half + i)
+                g = block // GROUP_BLOCKS + 1
+                if half == 0 and block % GROUP_BLOCKS == 0 and g < FULL_GROUPS:
+                    pieces += full_group_pieces(g, loop_planes)
+            if block > 1 and half == 0:
+                find_max(block - 2)
+            while done < len(units) and done * total_turns < (turn + 1) * len(units):
+                units[done]()
+                done += 1
+            before = block - 1
+            if block > 0:
+                for i in range(2):
+                    score_step(
+                        before,
+                        q_diag[before % 2],
+                        supers[before // 2][0],
+                        (2 * half + i) * BANK_MATMULS,
+                    )
+            for piece in pieces[:2]:
                 piece()
+            pieces = pieces[2:]
+            if block > 0 and half == 1 and block % GROUP_BLOCKS == 0:
+                end = block * BLOCK_T
+                pieces += finish_pieces(end - P, end, 0)
+        find_max(BLOCKS - 1)
+        for piece in pieces + finish_pieces(FULL_GROUPS * P, TENSOR_T, HALF):
+            piece()

@@ -91,6 +91,12 @@ def tile_differentialattention_pa_t_kernel(tc, x, Wq, Wk, lq1, lq2, lk1, lk2, ou
         ident = keep.tile([P, P], F32)
         make_identity(nc, ident[:])
 
+        q_diag = []
+        for turn in range(2):
+            diag = keep.tile([P, BLOCK_T, PAIRS, 2, ROWS], F32, name="q_diag%d" % turn)
+            nc.vector.memset(diag[:].rearrange("p t n s r -> p (t n s r)").bitcast(I32), 0)
+            q_diag.append(diag)
+
         dense_flat = keep.tile([P, TENSOR_T * ROWS], F32, align_bytes=64)
         dense = dense_flat[:].rearrange("p (m t) -> p m t", t=TENSOR_T)
         w_words = {}
@@ -111,14 +117,12 @@ def tile_differentialattention_pa_t_kernel(tc, x, Wq, Wk, lq1, lq2, lk1, lk2, ou
             w_scales[w] = keep.tile([P, W_COLS], U8, name="scales_%d" % w, align_bytes=64)
             w_padded[w] = keep.tile([P, PADDED], U32, name="padded_%d" % w, align_bytes=64)
             w_padded_scales[w] = keep.tile([P, PADDED], U8, name="padded_scales_%d" % w, align_bytes=64)
-            nc.gpsimd.memset(w_padded[w][:].bitcast(I32), 0)
-            nc.gpsimd.memset(w_padded_scales[w][:].bitcast(I32), 0)
-
-        q_diag = []
-        for turn in range(2):
-            diag = keep.tile([P, BLOCK_T, PAIRS, 2, ROWS], F32, name="q_diag%d" % turn)
-            nc.vector.memset(diag[:], 0.0)
-            q_diag.append(diag)
+            for wide, words in ((w_padded[w], D), (w_padded_scales[w], D // 4)):
+                gaps = wide[:].bitcast(I32)[:, : 2 * ROWS * words].rearrange(
+                    "p (r z w) -> p r z w", z=2, w=words
+                )
+                nc.gpsimd.memset(gaps[:, :, 0, :], 0)
+                nc.gpsimd.memset(wide[:].bitcast(I32)[:, 2 * ROWS * words :], 0)
 
         def copy_out(index, **operands):
             if index % 2 == 0:
@@ -214,7 +218,7 @@ def tile_differentialattention_pa_t_kernel(tc, x, Wq, Wk, lq1, lq2, lk1, lk2, ou
                     nc.scalar.copy(
                         out=by_run[:, first : first + 3 : 2], in_=by_time[:, :, LAST_T:, :]
                     )
-                    nc.vector.tensor_copy(
+                    nc.scalar.copy(
                         out=by_super[:, 0, s, h],
                         in_=planes[:].rearrange("p u (n t) -> p t n u", n=2)[:, :SUPER_T],
                     )
@@ -349,30 +353,26 @@ def tile_differentialattention_pa_t_kernel(tc, x, Wq, Wk, lq1, lq2, lk1, lk2, ou
                 negate=True,
             )
 
-        def finish_pieces(first_new, end, lo):
+        def take_max_off(block):
+            first = block * BLOCK_T
+            new = slice(first, first + block_times(block))
+            shape = [P, ROWS, block_times(block)]
+            nc.gpsimd.tensor_tensor(
+                out=dense[:, :, new],
+                in0=dense[:, :, new],
+                in1=neg_max[:, new].unsqueeze(1).to_broadcast(shape),
+                op=ALU.add,
+            )
+
+        def finish_pieces(first_new, end, lo, engine):
             first = end - P
             exps = tensor_way.tile([P, P, ROWS], F32, bufs=2)
 
             def turn_and_exp(m0):
                 flipped = psum_t.tile([P, BANK_ROWS, P], F32, tag="planes")
                 for i in range(BANK_ROWS):
-                    m = m0 + i
-                    if m > 0:
-                        nc.tensor.matmul(
-                            out=flipped[:, i, :],
-                            lhsT=dense[:, m - 1, first:end],
-                            rhs=ident[:],
-                            start=True,
-                            stop=False,
-                            is_transpose=True,
-                        )
-                    nc.tensor.matmul(
-                        out=flipped[:, i, :],
-                        lhsT=neg_max[:, first:end],
-                        rhs=ident[:],
-                        start=(m == 0),
-                        stop=True,
-                        is_transpose=True,
+                    nc.tensor.transpose(
+                        flipped[:, i, :], dense[:, (m0 + i - 1) % ROWS, first:end], ident[:]
                     )
                 nc.scalar.activation(
                     out=exps[lo:, :, m0 : m0 + BANK_ROWS],
@@ -388,27 +388,24 @@ def tile_differentialattention_pa_t_kernel(tc, x, Wq, Wk, lq1, lq2, lk1, lk2, ou
                 row_sum = tensor_way.tile([P, P], F32, bufs=2)
                 nc.vector.tensor_reduce(out=row_sum[lo:], in_=exps[lo:], axis=AXIS_X, op=ALU.add)
                 nc.vector.reciprocal(out=factor[lo:], in_=row_sum[lo:])
+                engine.tensor_scalar(
+                    out=by_j[lo:, 1], in0=by_j[lo:, 1], scalar1=neg_lam[lo:, 0:1], scalar2=None,
+                    op0=ALU.mult,
+                )
 
             def combine():
                 by_parity = exps[:].rearrange("p (e j) (h i) -> p j i e h", j=2, i=2)
                 shape = [P - lo, RUNS * HEADS, HEADS]
                 result = tensor_way.tile([P, RUNS * HEADS, HEADS], F32)
                 odd_part = tensor_way.tile([P, RUNS * HEADS, HEADS], F32)
-                nc.vector.scalar_tensor_tensor(
-                    out=odd_part[lo:],
-                    in0=by_parity[lo:, 1, 1],
-                    scalar=neg_lam[lo:, 0:1],
-                    in1=by_j[lo:, 1].unsqueeze(2).to_broadcast(shape),
-                    op0=ALU.mult,
-                    op1=ALU.mult,
-                )
-                nc.vector.tensor_tensor(
-                    out=result[lo:],
-                    in0=by_parity[lo:, 0, 0],
-                    in1=by_j[lo:, 0].unsqueeze(2).to_broadcast(shape),
-                    op=ALU.mult,
-                )
-                nc.vector.tensor_tensor(
+                for j, part in ((1, odd_part), (0, result)):
+                    engine.tensor_tensor(
+                        out=part[lo:],
+                        in0=by_parity[lo:, j, j],
+                        in1=by_j[lo:, j].unsqueeze(2).to_broadcast(shape),
+                        op=ALU.mult,
+                    )
+                engine.tensor_tensor(
                     out=result[lo:], in0=result[lo:], in1=odd_part[lo:], op=ALU.add
                 )
                 nc.sync.dma_start(
@@ -419,7 +416,7 @@ def tile_differentialattention_pa_t_kernel(tc, x, Wq, Wk, lq1, lq2, lk1, lk2, ou
                 )
 
             pieces = [lambda m0=m0: turn_and_exp(m0) for m0 in range(0, ROWS, BANK_ROWS)]
-            pieces += [find_factors, combine]
+            pieces += [find_factors, lambda: None, combine]
             return pieces
 
         def project_tile(w, bank_index, tile_index):
@@ -483,56 +480,76 @@ def tile_differentialattention_pa_t_kernel(tc, x, Wq, Wk, lq1, lq2, lk1, lk2, ou
             )
             return prod
 
-        def finish_batch(first_tile, tiles, batch):
+        def batch_stages(first_tile, tiles, batch):
             batch_rows = tiles * ROWS
             batch_shape = [P, batch_rows, ROWS]
             row_max = vector_way.tile([P, batch_rows], F32)
-            nc.vector.tensor_reduce(out=row_max[:], in_=batch[:], axis=AXIS_X, op=ALU.max)
-            nc.vector.tensor_tensor(
-                out=batch[:],
-                in0=batch[:],
-                in1=row_max[:].unsqueeze(2).to_broadcast(batch_shape),
-                op=ALU.subtract,
-            )
-            nc.scalar.activation(out=batch[:], in_=batch[:], func=ACT.Exp, scale=SCALE)
             row_sum = vector_way.tile([P, batch_rows], F32)
-            nc.vector.tensor_reduce(out=row_sum[:], in_=batch[:], axis=AXIS_X, op=ALU.add)
             factor = vector_way.tile([P, batch_rows], F32)
-            nc.vector.reciprocal(out=factor[:], in_=row_sum[:])
             odd_rows = factor[:].rearrange("p (e j) -> p e j", j=2)[:, :, 1]
-            nc.vector.tensor_scalar_mul(out=odd_rows, in0=odd_rows, scalar1=neg_lam[:, 0:1])
-            nc.vector.tensor_tensor(
-                out=batch[:],
-                in0=batch[:],
-                in1=factor[:].unsqueeze(2).to_broadcast(batch_shape),
-                op=ALU.mult,
-            )
-            by_parity = batch[:].rearrange("p (e j) (h i) -> p e j h i", j=2, i=2)
-            result = vector_way.tile([P, tiles * HEADS, HEADS], F32)
-            nc.vector.tensor_tensor(
-                out=result[:], in0=by_parity[:, :, 0, :, 0], in1=by_parity[:, :, 1, :, 1], op=ALU.add
-            )
-            by_run = out_rows.rearrange("(t y) e -> y t e", y=RUNS)
-            for v in range(tiles):
-                at = (first_tile + v) * P
-                stop = at + P
-                p0 = 0
-                while at < stop:
-                    y, t = divmod(at, VECTOR_T)
-                    count = min(VECTOR_T - t, stop - at)
-                    nc.sync.dma_start(
-                        out=by_run[y, TENSOR_T + t : TENSOR_T + t + count, :],
-                        in_=result[p0 : p0 + count, v * HEADS : (v + 1) * HEADS, :].rearrange(
-                            "p a h -> p (a h)"
-                        ),
-                    )
-                    at += count
-                    p0 += count
+
+            def find_row_max():
+                nc.vector.tensor_reduce(out=row_max[:], in_=batch[:], axis=AXIS_X, op=ALU.max)
+
+            def take_off():
+                nc.gpsimd.tensor_tensor(
+                    out=batch[:],
+                    in0=batch[:],
+                    in1=row_max[:].unsqueeze(2).to_broadcast(batch_shape),
+                    op=ALU.subtract,
+                )
+
+            def exponentiate():
+                nc.scalar.activation(out=batch[:], in_=batch[:], func=ACT.Exp, scale=SCALE)
+
+            def find_row_factors():
+                nc.vector.tensor_reduce(out=row_sum[:], in_=batch[:], axis=AXIS_X, op=ALU.add)
+                nc.vector.reciprocal(out=factor[:], in_=row_sum[:])
+
+            def scale_rows():
+                nc.gpsimd.tensor_scalar(
+                    out=odd_rows, in0=odd_rows, scalar1=neg_lam[:, 0:1], scalar2=None, op0=ALU.mult
+                )
+                nc.gpsimd.tensor_tensor(
+                    out=batch[:],
+                    in0=batch[:],
+                    in1=factor[:].unsqueeze(2).to_broadcast(batch_shape),
+                    op=ALU.mult,
+                )
+
+            def store():
+                by_parity = batch[:].rearrange("p (e j) (h i) -> p e j h i", j=2, i=2)
+                result = vector_way.tile([P, tiles * HEADS, HEADS], F32)
+                nc.gpsimd.tensor_tensor(
+                    out=result[:],
+                    in0=by_parity[:, :, 0, :, 0],
+                    in1=by_parity[:, :, 1, :, 1],
+                    op=ALU.add,
+                )
+                by_run = out_rows.rearrange("(t y) e -> y t e", y=RUNS)
+                for v in range(tiles):
+                    at = (first_tile + v) * P
+                    stop = at + P
+                    p0 = 0
+                    while at < stop:
+                        y, t = divmod(at, VECTOR_T)
+                        count = min(VECTOR_T - t, stop - at)
+                        nc.sync.dma_start(
+                            out=by_run[y, TENSOR_T + t : TENSOR_T + t + count, :],
+                            in_=result[p0 : p0 + count, v * HEADS : (v + 1) * HEADS, :].rearrange(
+                                "p a h -> p (a h)"
+                            ),
+                        )
+                        at += count
+                        p0 += count
+
+            return [find_row_max, take_off, exponentiate, find_row_factors, scale_rows, store]
 
         BATCHES = ((0, 3), (3, 2))
         tiles_open = {}
         scores_of = {}
         waiting = []
+        stages = []
 
         def sum_oldest():
             prod, tile_index, r = waiting.pop(0)
@@ -542,7 +559,11 @@ def tile_differentialattention_pa_t_kernel(tc, x, Wq, Wk, lq1, lq2, lk1, lk2, ou
             if r == ROWS - 1:
                 for first_tile, tiles in BATCHES:
                     if tile_index == first_tile + tiles - 1:
-                        finish_batch(first_tile, tiles, scores_of["batch", first_tile])
+                        stages.extend(batch_stages(first_tile, tiles, scores_of["batch", first_tile]))
+
+        def next_stage():
+            if stages:
+                stages.pop(0)()
 
         def open_k(tile_index):
             tiles_open[tile_index] = open_tile(tile_index)
@@ -560,6 +581,7 @@ def tile_differentialattention_pa_t_kernel(tc, x, Wq, Wk, lq1, lq2, lk1, lk2, ou
                 waiting.append((prod, tile_index, r))
 
         def row_unit(tile_index, r):
+            next_stage()
             q_sb, k_sb = tiles_open[tile_index]
             waiting.append((multiply_row(nc.gpsimd, q_sb[:, r, :], k_sb), tile_index, r))
             if tile_index + 1 < VECTOR_TILES and r == ROWS - 5:
@@ -574,7 +596,7 @@ def tile_differentialattention_pa_t_kernel(tc, x, Wq, Wk, lq1, lq2, lk1, lk2, ou
             for v in range(VECTOR_TILES)
             for r in range(VECTOR_ROWS, ROWS)
         ]
-        units += [sum_oldest] * SUM_LAG
+        units += [sum_oldest] * SUM_LAG + [next_stage] * 6
 
         LEAD = 2
         total_turns = 2 * BLOCKS
@@ -592,10 +614,10 @@ def tile_differentialattention_pa_t_kernel(tc, x, Wq, Wk, lq1, lq2, lk1, lk2, ou
         quantise_tiles(0, 2)
         open_k(0)
         open_q(0)
+        pad_weights(1)
         for piece in full_group_pieces(0, head_planes):
             piece()
-        for w in (1, 0):
-            pad_weights(w)
+        pad_weights(0)
         for turn in range(LEAD):
             k_turn(turn)
         quantise_tiles(2, 2)
@@ -618,6 +640,8 @@ def tile_differentialattention_pa_t_kernel(tc, x, Wq, Wk, lq1, lq2, lk1, lk2, ou
             while done < len(units) and done * total_turns < (turn + 1) * len(units):
                 units[done]()
                 done += 1
+            if block > 1 and half == 0:
+                take_max_off(block - 2)
             before = block - 1
             if block > 0:
                 for i in range(2):
@@ -630,9 +654,10 @@ def tile_differentialattention_pa_t_kernel(tc, x, Wq, Wk, lq1, lq2, lk1, lk2, ou
             for piece in pieces[:2]:
                 piece()
             pieces = pieces[2:]
-            if block > 0 and half == 1 and block % GROUP_BLOCKS == 0:
-                end = block * BLOCK_T
-                pieces += finish_pieces(end - P, end, 0)
+            if block > 1 and half == 0 and block % GROUP_BLOCKS == 1:
+                end = (block - 1) * BLOCK_T
+                pieces += finish_pieces(end - P, end, 0, nc.gpsimd)
         find_max(BLOCKS - 1)
-        for piece in pieces + finish_pieces(FULL_GROUPS * P, TENSOR_T, HALF):
+        take_max_off(BLOCKS - 1)
+        for piece in pieces + finish_pieces(FULL_GROUPS * P, TENSOR_T, HALF, nc.vector):
             piece()

@@ -56,7 +56,8 @@ W_COLS = ROWS * D
 PADDED = 2 * W_COLS + D
 TILE_ROWS = BANK // D
 
-VECTOR_ROWS = 1
+VECTOR_ROWS = (2, 1)
+STAGE_GAP = 3
 SUM_LAG = 2
 
 FLOPS = 2 * TOKENS * C * 2 * ROWS * D + 2 * TOKENS * ROWS * ROWS * D
@@ -82,7 +83,7 @@ def tile_differentialattention_pa_t_kernel(tc, x, Wq, Wk, lq1, lq2, lk1, lk2, ou
         tc.tile_pool(name="stage", bufs=2) as stage,
         tc.tile_pool(name="tensor_way", bufs=1) as tensor_way,
         tc.tile_pool(name="vector_way", bufs=2) as vector_way,
-        tc.tile_pool(name="products", bufs=4) as products,
+        tc.tile_pool(name="products", bufs=6) as products,
         tc.psum_pool(name="psum_t", bufs=2) as psum_t,
         tc.psum_pool(name="psum_y", bufs=4) as psum_y,
         tc.psum_pool(name="psum_s", bufs=2) as psum_s,
@@ -112,7 +113,7 @@ def tile_differentialattention_pa_t_kernel(tc, x, Wq, Wk, lq1, lq2, lk1, lk2, ou
         w_scales = {}
         w_padded = {}
         w_padded_scales = {}
-        for w in range(2):
+        for w in (1, 0):
             w_codes[w] = keep.tile([P, W_COLS], U32, name="codes_%d" % w, align_bytes=64)
             w_scales[w] = keep.tile([P, W_COLS], U8, name="scales_%d" % w, align_bytes=64)
             w_padded[w] = keep.tile([P, PADDED], U32, name="padded_%d" % w, align_bytes=64)
@@ -138,30 +139,57 @@ def tile_differentialattention_pa_t_kernel(tc, x, Wq, Wk, lq1, lq2, lk1, lk2, ou
                 return psum_t.tile([P, 2, 2 * P], F32, name="planes", tag="planes")
             return psum_y.tile([P, 2, 2 * P], F32, name="planes", tag="y")
 
-        for w, W in ((1, Wk), (0, Wq)):
-            by_row = w_words[w].rearrange("p (a j d u) -> p a j d u", a=HEADS, j=2, d=D)
-            for part in range(2):
-                w_sb = products.tile([P, HEADS // 2 * C], BF16, tag="prod")
-                nc.sync.dma_start(
-                    out=w_sb[:].rearrange("p (a c) -> p a c", c=C),
-                    in_=W[part * 512 : (part + 1) * 512, :].rearrange("(a p) c -> p a c", p=P),
-                )
-                w_f32 = w_sb[:].bitcast(F32)
-                for pair in range(2):
-                    a0 = part * HEADS // 2 + 2 * pair
-                    planes = head_planes()
-                    transpose_words(nc, planes, ident, w_f32, (2 * pair, 2 * pair + 1))
-                    by_j = planes[:].rearrange("p u (a d j) -> p j a d u", a=2, j=2)
-                    for j in range(2):
-                        copy_out(pair, out=by_row[:, a0 : a0 + 2, j], in_=by_j[:, j])
-                cols = slice(part * W_COLS // 2, (part + 1) * W_COLS // 2)
-                nc.vector.quantize_mx(
-                    out=w_codes[w][:, cols].bitcast(FP8X4),
-                    scales=w_scales[w][:, cols],
-                    in_=w_words[w][:, part * W_COLS : (part + 1) * W_COLS].bitcast(BF16),
-                )
+        w_loaded = {}
+        x_words = {}
 
-        def pad_weights(w):
+        def load_weight_part(w, W, part):
+            w_sb = products.tile([P, HEADS // 2 * C], BF16, tag="prod")
+            nc.sync.dma_start(
+                out=w_sb[:].rearrange("p (a c) -> p a c", c=C),
+                in_=W[part * 512 : (part + 1) * 512, :].rearrange("(a p) c -> p a c", p=P),
+            )
+            w_loaded[w, part] = w_sb[:].bitcast(F32)
+
+        def load_group(g):
+            x_sb = stage.tile([P, RUNS * C], BF16, tag="loaded", bufs=2)
+            nc.sync.dma_start(
+                out=x_sb[:],
+                in_=x_rows[g * GROUP_TOKENS : (g + 1) * GROUP_TOKENS, :].rearrange(
+                    "(t y) c -> t (y c)", y=RUNS
+                ),
+            )
+            x_words[g] = x_sb[:].bitcast(F32)
+
+        load_weight_part(1, Wk, 0)
+        load_group(0)
+        load_weight_part(1, Wk, 1)
+        load_weight_part(0, Wq, 0)
+        load_weight_part(0, Wq, 1)
+        load_group(GROUPS - 1)
+        vectors = keep.tile([P, 4, D], BF16)
+        for v, vector in enumerate((lq1, lq2, lk1, lk2)):
+            nc.sync.dma_start(out=vectors[:, v, :], in_=vector.partition_broadcast(P))
+
+        def turn_weight_part(w, part):
+            by_row = w_words[w].rearrange("p (a j d u) -> p a j d u", a=HEADS, j=2, d=D)
+            for pair in range(2):
+                a0 = part * HEADS // 2 + 2 * pair
+                planes = head_planes()
+                transpose_words(nc, planes, ident, w_loaded[w, part], (2 * pair, 2 * pair + 1))
+                by_j = planes[:].rearrange("p u (a d j) -> p j a d u", a=2, j=2)
+                for j in range(2):
+                    copy_out(pair, out=by_row[:, a0 : a0 + 2, j], in_=by_j[:, j])
+
+        def quantise_weight_part(w, part):
+            cols = slice(part * W_COLS // 2, (part + 1) * W_COLS // 2)
+            nc.vector.quantize_mx(
+                out=w_codes[w][:, cols].bitcast(FP8X4),
+                scales=w_scales[w][:, cols],
+                in_=w_words[w][:, part * W_COLS : (part + 1) * W_COLS].bitcast(BF16),
+            )
+
+        def pad_weight_part(w, part):
+            rows = slice(part * ROWS // 2, (part + 1) * ROWS // 2)
             for narrow, wide, words in (
                 (w_codes[w], w_padded[w], D),
                 (w_scales[w], w_padded_scales[w], D // 4),
@@ -169,8 +197,8 @@ def tile_differentialattention_pa_t_kernel(tc, x, Wq, Wk, lq1, lq2, lk1, lk2, ou
                 nc.vector.tensor_copy(
                     out=wide[:].bitcast(I32)[:, words:].rearrange(
                         "p (r z w) -> p r z w", z=2, w=words
-                    )[:, :, 0, :],
-                    in_=narrow[:].bitcast(I32).rearrange("p (r w) -> p r w", w=words),
+                    )[:, rows, 0, :],
+                    in_=narrow[:].bitcast(I32).rearrange("p (r w) -> p r w", w=words)[:, rows],
                 )
 
         x_codes = keep.tile([P, X_COLS], U32, align_bytes=64)
@@ -181,21 +209,6 @@ def tile_differentialattention_pa_t_kernel(tc, x, Wq, Wk, lq1, lq2, lk1, lk2, ou
             nc.vector.quantize_mx(
                 out=x_codes[:, cols].bitcast(FP8X4), scales=x_scales[:, cols], in_=grouped
             )
-
-        vectors = keep.tile([P, 4, D], BF16)
-        x_words = {}
-        for g in [GROUPS - 1] + list(range(FULL_GROUPS)):
-            if g == 1:
-                for v, vector in enumerate((lq1, lq2, lk1, lk2)):
-                    nc.sync.dma_start(out=vectors[:, v, :], in_=vector.partition_broadcast(P))
-            x_sb = stage.tile([P, RUNS * C], BF16, tag="loaded", bufs=2)
-            nc.sync.dma_start(
-                out=x_sb[:],
-                in_=x_rows[g * GROUP_TOKENS : (g + 1) * GROUP_TOKENS, :].rearrange(
-                    "(t y) c -> t (y c)", y=RUNS
-                ),
-            )
-            x_words[g] = x_sb[:].bitcast(F32)
 
         def super_view(words):
             return words.rearrange(
@@ -229,7 +242,7 @@ def tile_differentialattention_pa_t_kernel(tc, x, Wq, Wk, lq1, lq2, lk1, lk2, ou
                 vec_words[:, 2 * first * P : 2 * (first + tiles) * P].bitcast(BF16),
             )
 
-        def full_group_pieces(g, new_planes):
+        def full_group_pieces(g, new_planes, copy):
             grouped = stage.tile([P, 4 * GROUP_TOKENS], BF16, tag="grouped", bufs=1, align_bytes=64)
             by_super = super_view(grouped[:].bitcast(F32))
 
@@ -237,14 +250,30 @@ def tile_differentialattention_pa_t_kernel(tc, x, Wq, Wk, lq1, lq2, lk1, lk2, ou
                 planes = new_planes()
                 turn_runs(x_words[g], planes, s, h)
                 for b in range(2):
-                    nc.scalar.copy(
+                    copy(
+                        h,
                         out=by_super[:, b, s, h],
                         in_=planes[:].rearrange("p u (n b t) -> p b t n u", n=2, b=2)[:, b],
                     )
 
+            def quantise(b):
+                first = b * SUPER_COLS
+                quantise_x(
+                    g * GROUP_TOKENS + first, grouped[:, 4 * first : 4 * (first + SUPER_COLS)]
+                )
+
             pieces = [lambda s=s, h=h: turn(s, h) for s in range(2) for h in range(2)]
-            pieces.append(lambda: quantise_x(g * GROUP_TOKENS, grouped[:]))
+            pieces += [lambda b=b: quantise(b) for b in range(2)]
             return pieces
+
+        def scalar_copy(index, **operands):
+            nc.scalar.copy(**operands)
+
+        def loop_bank():
+            return psum_t.tile([P, BANK_ROWS, P], F32, name="flipped", tag="planes")
+
+        def last_bank():
+            return psum_y.tile([P, BANK_ROWS, P], F32, name="flipped", tag="y")
 
         def loop_planes():
             return psum_t.tile([P, 2, 2 * P], F32, name="planes", tag="planes")
@@ -254,12 +283,16 @@ def tile_differentialattention_pa_t_kernel(tc, x, Wq, Wk, lq1, lq2, lk1, lk2, ou
         lam_exps = keep.tile([P, 2], F32)
         neg_lam = keep.tile([P, 1], F32)
 
-        def find_lam():
+        def find_lam_dots():
             nc.vector.tensor_tensor(
                 out=lam_products[:], in0=vectors[:, 0:2, :], in1=vectors[:, 2:4, :], op=ALU.mult
             )
             nc.vector.tensor_reduce(out=lam_dots[:], in_=lam_products[:], axis=AXIS_X, op=ALU.add)
+
+        def find_lam_exps():
             nc.scalar.activation(out=lam_exps[:], in_=lam_dots[:], func=ACT.Exp)
+
+        def find_neg_lam():
             nc.vector.tensor_tensor(
                 out=neg_lam[:], in0=lam_exps[:, 1:2], in1=lam_exps[:, 0:1], op=ALU.subtract
             )
@@ -353,70 +386,97 @@ def tile_differentialattention_pa_t_kernel(tc, x, Wq, Wk, lq1, lq2, lk1, lk2, ou
                 negate=True,
             )
 
-        def take_max_off(block):
+        def take_max_off(block, engine):
             first = block * BLOCK_T
             new = slice(first, first + block_times(block))
             shape = [P, ROWS, block_times(block)]
-            nc.gpsimd.tensor_tensor(
+            engine.tensor_tensor(
                 out=dense[:, :, new],
                 in0=dense[:, :, new],
                 in1=neg_max[:, new].unsqueeze(1).to_broadcast(shape),
                 op=ALU.add,
             )
 
-        def finish_pieces(first_new, end, lo, engine):
+        def finish_pieces(first_new, end, lo, engines, new_bank):
             first = end - P
-            exps = tensor_way.tile([P, P, ROWS], F32, bufs=2)
+            runs = RUNS // len(engines)
+            loaded = stage.tile([P, RUNS * C], BF16, tag="loaded", bufs=2)
+            exps = loaded[:].bitcast(F32).rearrange("p (e m) -> p e m", m=ROWS)
+            factor = tensor_way.tile([P, P], F32, bufs=2)
+            row_sum = tensor_way.tile([P, P], F32, bufs=2)
+            result = tensor_way.tile([P, RUNS * HEADS, HEADS], F32)
+            odd_part = tensor_way.tile([P, RUNS * HEADS, HEADS], F32)
+            by_j = factor[:].rearrange("p (e j) -> p j e", j=2)
+            banks = {}
 
-            def turn_and_exp(m0):
-                flipped = psum_t.tile([P, BANK_ROWS, P], F32, tag="planes")
+            def turn(m0):
+                flipped = new_bank()
                 for i in range(BANK_ROWS):
                     nc.tensor.transpose(
                         flipped[:, i, :], dense[:, (m0 + i - 1) % ROWS, first:end], ident[:]
                     )
+                banks[m0] = flipped
+
+            def rows_of(part):
+                return slice(part * runs * ROWS, (part + 1) * runs * ROWS)
+
+            def exponentiate(m0, part):
+                rows = rows_of(part)
                 nc.scalar.activation(
-                    out=exps[lo:, :, m0 : m0 + BANK_ROWS],
-                    in_=flipped[lo:].rearrange("p i e -> p e i"),
+                    out=exps[lo:, rows, m0 : m0 + BANK_ROWS],
+                    in_=banks[m0][lo:, :, rows].rearrange("p i e -> p e i"),
                     func=ACT.Exp,
                     scale=SCALE,
                 )
 
-            factor = tensor_way.tile([P, P], F32, bufs=2)
-            by_j = factor[:].rearrange("p (e j) -> p j e", j=2)
-
-            def find_factors():
-                row_sum = tensor_way.tile([P, P], F32, bufs=2)
-                nc.vector.tensor_reduce(out=row_sum[lo:], in_=exps[lo:], axis=AXIS_X, op=ALU.add)
-                nc.vector.reciprocal(out=factor[lo:], in_=row_sum[lo:])
-                engine.tensor_scalar(
-                    out=by_j[lo:, 1], in0=by_j[lo:, 1], scalar1=neg_lam[lo:, 0:1], scalar2=None,
-                    op0=ALU.mult,
+            def find_factors(part):
+                rows = rows_of(part)
+                nc.vector.tensor_reduce(
+                    out=row_sum[lo:, rows], in_=exps[lo:, rows], axis=AXIS_X, op=ALU.add
                 )
+                nc.vector.reciprocal(out=factor[lo:, rows], in_=row_sum[lo:, rows])
 
-            def combine():
-                by_parity = exps[:].rearrange("p (e j) (h i) -> p j i e h", j=2, i=2)
-                shape = [P - lo, RUNS * HEADS, HEADS]
-                result = tensor_way.tile([P, RUNS * HEADS, HEADS], F32)
-                odd_part = tensor_way.tile([P, RUNS * HEADS, HEADS], F32)
-                for j, part in ((1, odd_part), (0, result)):
+            def combine(part):
+                engine = engines[part]
+                heads = slice(part * runs * HEADS, (part + 1) * runs * HEADS)
+                engine.tensor_scalar(
+                    out=by_j[lo:, 1, heads], in0=by_j[lo:, 1, heads], scalar1=neg_lam[lo:, 0:1],
+                    scalar2=None, op0=ALU.mult,
+                )
+                by_parity = exps.rearrange("p (e j) (h i) -> p j i e h", j=2, i=2)
+                shape = [P - lo, runs * HEADS, HEADS]
+                for j, half in ((1, odd_part), (0, result)):
                     engine.tensor_tensor(
-                        out=part[lo:],
-                        in0=by_parity[lo:, j, j],
-                        in1=by_j[lo:, j].unsqueeze(2).to_broadcast(shape),
+                        out=half[lo:, heads],
+                        in0=by_parity[lo:, j, j, heads],
+                        in1=by_j[lo:, j, heads].unsqueeze(2).to_broadcast(shape),
                         op=ALU.mult,
                     )
                 engine.tensor_tensor(
-                    out=result[lo:], in0=result[lo:], in1=odd_part[lo:], op=ALU.add
+                    out=result[lo:, heads], in0=result[lo:, heads], in1=odd_part[lo:, heads],
+                    op=ALU.add,
                 )
                 nc.sync.dma_start(
                     out=out_rows[first_new * RUNS : end * RUNS, :].rearrange(
-                        "(t y) e -> t (y e)", y=RUNS
+                        "(t y) e -> t y e", y=RUNS
+                    )[:, part * runs : (part + 1) * runs],
+                    in_=result[first_new - first :, heads].rearrange(
+                        "p (y a) h -> p y (a h)", a=HEADS
                     ),
-                    in_=result[first_new - first :].rearrange("p e h -> p (e h)"),
                 )
 
-            pieces = [lambda m0=m0: turn_and_exp(m0) for m0 in range(0, ROWS, BANK_ROWS)]
-            pieces += [find_factors, lambda: None, combine]
+            def turn_and_exponentiate(m0):
+                turn(m0)
+                exponentiate(m0, 0)
+
+            steps = range(0, ROWS, BANK_ROWS)
+            pieces = [lambda m0=m0: turn_and_exponentiate(m0) for m0 in steps]
+            if len(engines) == 1:
+                return pieces + [lambda: find_factors(0), lambda: None, lambda: combine(0)]
+            for part in range(1, len(engines)):
+                pieces += [lambda m0=m0, part=part: exponentiate(m0, part) for m0 in steps]
+            pieces += [lambda part=part: find_factors(part) for part in range(len(engines))]
+            pieces += [lambda part=part: combine(part) for part in range(len(engines))]
             return pieces
 
         def project_tile(w, bank_index, tile_index):
@@ -461,13 +521,14 @@ def tile_differentialattention_pa_t_kernel(tc, x, Wq, Wk, lq1, lq2, lk1, lk2, ou
             made = []
             for bank_index in range(ROWS // TILE_ROWS):
                 bank = project_tile(0, bank_index, tile_index)
-                skip = VECTOR_ROWS if bank_index == 0 else 0
+                skip = VECTOR_ROWS[bank_index]
                 nc.scalar.copy(
                     out=q_sb[:, bank_index * TILE_ROWS + skip : (bank_index + 1) * TILE_ROWS, :],
                     in_=bank[:, skip:],
                 )
                 for r in range(skip):
-                    made.append(multiply_row(nc.vector, bank[:, r, :], k_sb))
+                    prod = multiply_row(nc.vector, bank[:, r, :], k_sb)
+                    made.append((prod, tile_index, bank_index * TILE_ROWS + r))
             return made
 
         def multiply_row(engine, q_row, k_sb):
@@ -561,8 +622,8 @@ def tile_differentialattention_pa_t_kernel(tc, x, Wq, Wk, lq1, lq2, lk1, lk2, ou
                     if tile_index == first_tile + tiles - 1:
                         stages.extend(batch_stages(first_tile, tiles, scores_of["batch", first_tile]))
 
-        def next_stage():
-            if stages:
+        def next_stage(unit):
+            if stages and unit % STAGE_GAP == 0:
                 stages.pop(0)()
 
         def open_k(tile_index):
@@ -577,11 +638,10 @@ def tile_differentialattention_pa_t_kernel(tc, x, Wq, Wk, lq1, lq2, lk1, lk2, ou
             fill_k(tile_index, tiles_open[tile_index])
 
         def open_q(tile_index):
-            for r, prod in enumerate(fill_q(tile_index, tiles_open[tile_index])):
-                waiting.append((prod, tile_index, r))
+            waiting.extend(fill_q(tile_index, tiles_open[tile_index]))
 
         def row_unit(tile_index, r):
-            next_stage()
+            next_stage(r)
             q_sb, k_sb = tiles_open[tile_index]
             waiting.append((multiply_row(nc.gpsimd, q_sb[:, r, :], k_sb), tile_index, r))
             if tile_index + 1 < VECTOR_TILES and r == ROWS - 5:
@@ -594,9 +654,10 @@ def tile_differentialattention_pa_t_kernel(tc, x, Wq, Wk, lq1, lq2, lk1, lk2, ou
         units = [
             lambda v=v, r=r: row_unit(v, r)
             for v in range(VECTOR_TILES)
-            for r in range(VECTOR_ROWS, ROWS)
+            for r in range(ROWS)
+            if r % TILE_ROWS >= VECTOR_ROWS[r // TILE_ROWS]
         ]
-        units += [sum_oldest] * SUM_LAG + [next_stage] * 6
+        units += [sum_oldest] * SUM_LAG + [lambda: next_stage(0)] * 6
 
         LEAD = 2
         total_turns = 2 * BLOCKS
@@ -610,20 +671,35 @@ def tile_differentialattention_pa_t_kernel(tc, x, Wq, Wk, lq1, lq2, lk1, lk2, ou
                 for i in range(2):
                     k_step(index, supers[index], 2 * quarter + i)
 
+        turn_weight_part(1, 0)
+        quantise_weight_part(1, 0)
+        first_group = full_group_pieces(0, head_planes, copy_out)
+        for piece in first_group[:4]:
+            piece()
+        load_group(1)
+        pad_weight_part(1, 0)
+        first_group[4]()
+        turn_weight_part(1, 1)
+        k_turn(0)
+        quantise_weight_part(1, 1)
+        pad_weight_part(1, 1)
+        turn_weight_part(0, 0)
+        quantise_weight_part(0, 0)
+        k_turn(1)
+        turn_weight_part(0, 1)
+        quantise_weight_part(0, 1)
         prepare_last_group()
+        load_group(2)
         quantise_tiles(0, 2)
+        pad_weight_part(0, 0)
+        pad_weight_part(0, 1)
         open_k(0)
         open_q(0)
-        pad_weights(1)
-        for piece in full_group_pieces(0, head_planes):
-            piece()
-        pad_weights(0)
-        for turn in range(LEAD):
-            k_turn(turn)
+        first_group[5]()
         quantise_tiles(2, 2)
         quantise_tiles(4, 1)
         quantise_x(FULL_GROUPS * GROUP_TOKENS, last_words.bitcast(BF16))
-        find_lam()
+        find_lam_dots()
         pieces = []
         done = 0
         for turn in range(total_turns + 1):
@@ -634,14 +710,15 @@ def tile_differentialattention_pa_t_kernel(tc, x, Wq, Wk, lq1, lq2, lk1, lk2, ou
                     q_step(block, q_diag[block % 2], 2 * half + i)
                 g = block // GROUP_BLOCKS + 1
                 if half == 0 and block % GROUP_BLOCKS == 0 and g < FULL_GROUPS:
-                    pieces += full_group_pieces(g, loop_planes)
+                    pieces += full_group_pieces(g, loop_planes, scalar_copy)
             if block > 1 and half == 0:
                 find_max(block - 2)
-            while done < len(units) and done * total_turns < (turn + 1) * len(units):
+            share = max(turn, (turn + 1) / 2)
+            while done < len(units) and done * (total_turns - 1) < share * len(units):
                 units[done]()
                 done += 1
             if block > 1 and half == 0:
-                take_max_off(block - 2)
+                take_max_off(block - 2, nc.gpsimd)
             before = block - 1
             if block > 0:
                 for i in range(2):
@@ -656,8 +733,11 @@ def tile_differentialattention_pa_t_kernel(tc, x, Wq, Wk, lq1, lq2, lk1, lk2, ou
             pieces = pieces[2:]
             if block > 1 and half == 0 and block % GROUP_BLOCKS == 1:
                 end = (block - 1) * BLOCK_T
-                pieces += finish_pieces(end - P, end, 0, nc.gpsimd)
+                pieces += finish_pieces(end - P, end, 0, (nc.gpsimd,), loop_bank)
+            if turn == 2:
+                pieces += [find_lam_exps, find_neg_lam]
         find_max(BLOCKS - 1)
-        take_max_off(BLOCKS - 1)
-        for piece in pieces + finish_pieces(FULL_GROUPS * P, TENSOR_T, HALF, nc.vector):
+        take_max_off(BLOCKS - 1, nc.vector)
+        last = finish_pieces(FULL_GROUPS * P, TENSOR_T, HALF, (nc.gpsimd, nc.vector), last_bank)
+        for piece in pieces + last:
             piece()

@@ -84,8 +84,7 @@ def tile_differentialattention_pa_t_kernel(tc, x, Wq, Wk, lq1, lq2, lk1, lk2, ou
         tc.tile_pool(name="tensor_way", bufs=1) as tensor_way,
         tc.tile_pool(name="vector_way", bufs=2) as vector_way,
         tc.tile_pool(name="products", bufs=6) as products,
-        tc.psum_pool(name="psum_t", bufs=2) as psum_t,
-        tc.psum_pool(name="psum_y", bufs=4) as psum_y,
+        tc.psum_pool(name="psum_y", bufs=6) as psum_y,
         tc.psum_pool(name="psum_s", bufs=2) as psum_s,
         tc.manual_schedule(),
     ):
@@ -131,14 +130,6 @@ def tile_differentialattention_pa_t_kernel(tc, x, Wq, Wk, lq1, lq2, lk1, lk2, ou
             else:
                 nc.vector.tensor_copy(**operands)
 
-        head_banks = [0]
-
-        def head_planes():
-            head_banks[0] += 1
-            if head_banks[0] % 3 == 0:
-                return psum_t.tile([P, 2, 2 * P], F32, name="planes", tag="planes")
-            return psum_y.tile([P, 2, 2 * P], F32, name="planes", tag="y")
-
         w_loaded = {}
         x_words = {}
 
@@ -174,7 +165,7 @@ def tile_differentialattention_pa_t_kernel(tc, x, Wq, Wk, lq1, lq2, lk1, lk2, ou
             by_row = w_words[w].rearrange("p (a j d u) -> p a j d u", a=HEADS, j=2, d=D)
             for pair in range(2):
                 a0 = part * HEADS // 2 + 2 * pair
-                planes = head_planes()
+                planes = psum_y.tile([P, 2, 2 * P], F32, name="planes", tag="y")
                 transpose_words(nc, planes, ident, w_loaded[w, part], (2 * pair, 2 * pair + 1))
                 by_j = planes[:].rearrange("p u (a d j) -> p j a d u", a=2, j=2)
                 for j in range(2):
@@ -224,7 +215,7 @@ def tile_differentialattention_pa_t_kernel(tc, x, Wq, Wk, lq1, lq2, lk1, lk2, ou
             by_run = vec_words.rearrange("p (y t u) -> p y t u", y=RUNS, u=2)
             for h in range(2):
                 for s in range(2):
-                    planes = head_planes()
+                    planes = psum_y.tile([P, 2, 2 * P], F32, name="planes", tag="y")
                     turn_runs(x_words[GROUPS - 1], planes, s, h)
                     by_time = planes[:].rearrange("p u (n t) -> p n t u", n=2)
                     first = 4 * h + s
@@ -242,12 +233,12 @@ def tile_differentialattention_pa_t_kernel(tc, x, Wq, Wk, lq1, lq2, lk1, lk2, ou
                 vec_words[:, 2 * first * P : 2 * (first + tiles) * P].bitcast(BF16),
             )
 
-        def full_group_pieces(g, new_planes, copy):
+        def full_group_pieces(g, copy):
             grouped = stage.tile([P, 4 * GROUP_TOKENS], BF16, tag="grouped", bufs=1, align_bytes=64)
             by_super = super_view(grouped[:].bitcast(F32))
 
             def turn(s, h):
-                planes = new_planes()
+                planes = psum_y.tile([P, 2, 2 * P], F32, name="planes", tag="y")
                 turn_runs(x_words[g], planes, s, h)
                 for b in range(2):
                     copy(
@@ -268,15 +259,6 @@ def tile_differentialattention_pa_t_kernel(tc, x, Wq, Wk, lq1, lq2, lk1, lk2, ou
 
         def scalar_copy(index, **operands):
             nc.scalar.copy(**operands)
-
-        def loop_bank():
-            return psum_t.tile([P, BANK_ROWS, P], F32, name="flipped", tag="planes")
-
-        def last_bank():
-            return psum_y.tile([P, BANK_ROWS, P], F32, name="flipped", tag="y")
-
-        def loop_planes():
-            return psum_t.tile([P, 2, 2 * P], F32, name="planes", tag="planes")
 
         lam_products = keep.tile([P, 2, D], F32)
         lam_dots = keep.tile([P, 2], F32)
@@ -397,87 +379,119 @@ def tile_differentialattention_pa_t_kernel(tc, x, Wq, Wk, lq1, lq2, lk1, lk2, ou
                 op=ALU.add,
             )
 
-        def finish_pieces(first_new, end, lo, engines, new_bank):
+        def parts_of(factor):
+            return factor[:].rearrange("p (e j) -> p j e", j=2)
+
+        def store(first_new, end, result):
+            nc.sync.dma_start(
+                out=out_rows[first_new * RUNS : end * RUNS, :].rearrange(
+                    "(t y) e -> t (y e)", y=RUNS
+                ),
+                in_=result[P - (end - first_new) :].rearrange("p e h -> p (e h)"),
+            )
+
+        def finish_pieces(end):
             first = end - P
-            runs = RUNS // len(engines)
             loaded = stage.tile([P, RUNS * C], BF16, tag="loaded", bufs=2)
             exps = loaded[:].bitcast(F32).rearrange("p (e m) -> p e m", m=ROWS)
             factor = tensor_way.tile([P, P], F32, bufs=2)
-            row_sum = tensor_way.tile([P, P], F32, bufs=2)
-            result = tensor_way.tile([P, RUNS * HEADS, HEADS], F32)
-            odd_part = tensor_way.tile([P, RUNS * HEADS, HEADS], F32)
-            by_j = factor[:].rearrange("p (e j) -> p j e", j=2)
-            banks = {}
+            by_j = parts_of(factor)
 
-            def turn(m0):
-                flipped = new_bank()
+            def turn_and_exp(m0):
+                flipped = psum_y.tile([P, BANK_ROWS, P], F32, tag="y")
                 for i in range(BANK_ROWS):
                     nc.tensor.transpose(
                         flipped[:, i, :], dense[:, (m0 + i - 1) % ROWS, first:end], ident[:]
                     )
-                banks[m0] = flipped
-
-            def rows_of(part):
-                return slice(part * runs * ROWS, (part + 1) * runs * ROWS)
-
-            def exponentiate(m0, part):
-                rows = rows_of(part)
                 nc.scalar.activation(
-                    out=exps[lo:, rows, m0 : m0 + BANK_ROWS],
-                    in_=banks[m0][lo:, :, rows].rearrange("p i e -> p e i"),
+                    out=exps[:, :, m0 : m0 + BANK_ROWS],
+                    in_=flipped[:].rearrange("p i e -> p e i"),
                     func=ACT.Exp,
                     scale=SCALE,
                 )
 
-            def find_factors(part):
-                rows = rows_of(part)
-                nc.vector.tensor_reduce(
-                    out=row_sum[lo:, rows], in_=exps[lo:, rows], axis=AXIS_X, op=ALU.add
-                )
-                nc.vector.reciprocal(out=factor[lo:, rows], in_=row_sum[lo:, rows])
+            def find_factors():
+                row_sum = tensor_way.tile([P, P], F32, bufs=2)
+                nc.vector.tensor_reduce(out=row_sum[:], in_=exps, axis=AXIS_X, op=ALU.add)
+                nc.vector.reciprocal(out=factor[:], in_=row_sum[:])
 
-            def combine(part):
-                engine = engines[part]
-                heads = slice(part * runs * HEADS, (part + 1) * runs * HEADS)
-                engine.tensor_scalar(
-                    out=by_j[lo:, 1, heads], in0=by_j[lo:, 1, heads], scalar1=neg_lam[lo:, 0:1],
-                    scalar2=None, op0=ALU.mult,
+            def combine():
+                nc.gpsimd.tensor_scalar(
+                    out=by_j[:, 1], in0=by_j[:, 1], scalar1=neg_lam[:, 0:1], scalar2=None,
+                    op0=ALU.mult,
                 )
                 by_parity = exps.rearrange("p (e j) (h i) -> p j i e h", j=2, i=2)
-                shape = [P - lo, runs * HEADS, HEADS]
+                shape = [P, RUNS * HEADS, HEADS]
+                result = tensor_way.tile(shape, F32)
+                odd_part = tensor_way.tile(shape, F32)
                 for j, half in ((1, odd_part), (0, result)):
-                    engine.tensor_tensor(
-                        out=half[lo:, heads],
-                        in0=by_parity[lo:, j, j, heads],
-                        in1=by_j[lo:, j, heads].unsqueeze(2).to_broadcast(shape),
+                    nc.gpsimd.tensor_tensor(
+                        out=half[:],
+                        in0=by_parity[:, j, j],
+                        in1=by_j[:, j].unsqueeze(2).to_broadcast(shape),
                         op=ALU.mult,
                     )
-                engine.tensor_tensor(
-                    out=result[lo:, heads], in0=result[lo:, heads], in1=odd_part[lo:, heads],
+                nc.gpsimd.tensor_tensor(
+                    out=result[:], in0=result[:], in1=odd_part[:], op=ALU.add
+                )
+                store(first, end, result)
+
+            pieces = [lambda m0=m0: turn_and_exp(m0) for m0 in range(0, ROWS, BANK_ROWS)]
+            return pieces + [find_factors, lambda: None, combine]
+
+        def exponentiate_block(block):
+            first = block * BLOCK_T
+            new = slice(first, first + block_times(block))
+            nc.scalar.activation(
+                out=dense[:, :, new], in_=dense[:, :, new], func=ACT.Exp, scale=SCALE
+            )
+
+        def finish_last():
+            window = slice(TENSOR_T - P, TENSOR_T)
+            lo = HALF
+            sums = psum_y.tile([P, BANK_ROWS, P], F32, tag="y")
+            for m in range(ROWS):
+                nc.tensor.matmul(
+                    out=sums[:, 0, :],
+                    lhsT=dense[:, m, window],
+                    rhs=ident[:],
+                    start=(m == 0),
+                    stop=(m == ROWS - 1),
+                    is_transpose=True,
+                )
+            factor = tensor_way.tile([P, P], F32, bufs=2)
+            by_j = parts_of(factor)
+            nc.vector.reciprocal(out=factor[lo:], in_=sums[lo:, 0, :])
+            nc.vector.tensor_scalar(
+                out=by_j[lo:, 1], in0=by_j[lo:, 1], scalar1=neg_lam[lo:, 0:1], scalar2=None,
+                op0=ALU.mult,
+            )
+            result = tensor_way.tile([P, RUNS * HEADS, HEADS], F32)
+            odd_part = tensor_way.tile([P, RUNS * HEADS, HEADS], F32)
+            for h0 in range(0, HEADS, BANK_ROWS):
+                heads = slice(h0, h0 + BANK_ROWS)
+                for j, half in ((1, odd_part), (0, result)):
+                    flipped = psum_y.tile([P, BANK_ROWS, P], F32, tag="y")
+                    for i in range(BANK_ROWS):
+                        m = 2 * (h0 + i) + j
+                        nc.tensor.transpose(
+                            flipped[:, i, :], dense[:, (m - 1) % ROWS, window], ident[:]
+                        )
+                    nc.vector.tensor_tensor(
+                        out=half[lo:, :, heads],
+                        in0=flipped[lo:].rearrange("p i (e j) -> p j e i", j=2)[:, j],
+                        in1=by_j[lo:, j].unsqueeze(2).to_broadcast(
+                            [P - lo, RUNS * HEADS, BANK_ROWS]
+                        ),
+                        op=ALU.mult,
+                    )
+                nc.vector.tensor_tensor(
+                    out=result[lo:, :, heads],
+                    in0=result[lo:, :, heads],
+                    in1=odd_part[lo:, :, heads],
                     op=ALU.add,
                 )
-                nc.sync.dma_start(
-                    out=out_rows[first_new * RUNS : end * RUNS, :].rearrange(
-                        "(t y) e -> t y e", y=RUNS
-                    )[:, part * runs : (part + 1) * runs],
-                    in_=result[first_new - first :, heads].rearrange(
-                        "p (y a) h -> p y (a h)", a=HEADS
-                    ),
-                )
-
-            def turn_and_exponentiate(m0):
-                turn(m0)
-                exponentiate(m0, 0)
-
-            steps = range(0, ROWS, BANK_ROWS)
-            pieces = [lambda m0=m0: turn_and_exponentiate(m0) for m0 in steps]
-            if len(engines) == 1:
-                return pieces + [lambda: find_factors(0), lambda: None, lambda: combine(0)]
-            for part in range(1, len(engines)):
-                pieces += [lambda m0=m0, part=part: exponentiate(m0, part) for m0 in steps]
-            pieces += [lambda part=part: find_factors(part) for part in range(len(engines))]
-            pieces += [lambda part=part: combine(part) for part in range(len(engines))]
-            return pieces
+            store(FULL_GROUPS * P, TENSOR_T, result)
 
         def project_tile(w, bank_index, tile_index):
             bank = psum_y.tile([P, BANK], F32, tag="y")
@@ -604,7 +618,10 @@ def tile_differentialattention_pa_t_kernel(tc, x, Wq, Wk, lq1, lq2, lk1, lk2, ou
                         at += count
                         p0 += count
 
-            return [find_row_max, take_off, exponentiate, find_row_factors, scale_rows, store]
+            def pause():
+                pass
+
+            return [find_row_max, take_off, pause, exponentiate, find_row_factors, scale_rows, store]
 
         BATCHES = ((0, 3), (3, 2))
         tiles_open = {}
@@ -657,7 +674,7 @@ def tile_differentialattention_pa_t_kernel(tc, x, Wq, Wk, lq1, lq2, lk1, lk2, ou
             for r in range(ROWS)
             if r % TILE_ROWS >= VECTOR_ROWS[r // TILE_ROWS]
         ]
-        units += [sum_oldest] * SUM_LAG + [lambda: next_stage(0)] * 6
+        units += [sum_oldest] * SUM_LAG + [lambda: next_stage(0)] * 7
 
         LEAD = 2
         total_turns = 2 * BLOCKS
@@ -673,7 +690,7 @@ def tile_differentialattention_pa_t_kernel(tc, x, Wq, Wk, lq1, lq2, lk1, lk2, ou
 
         turn_weight_part(1, 0)
         quantise_weight_part(1, 0)
-        first_group = full_group_pieces(0, head_planes, copy_out)
+        first_group = full_group_pieces(0, copy_out)
         for piece in first_group[:4]:
             piece()
         load_group(1)
@@ -710,7 +727,7 @@ def tile_differentialattention_pa_t_kernel(tc, x, Wq, Wk, lq1, lq2, lk1, lk2, ou
                     q_step(block, q_diag[block % 2], 2 * half + i)
                 g = block // GROUP_BLOCKS + 1
                 if half == 0 and block % GROUP_BLOCKS == 0 and g < FULL_GROUPS:
-                    pieces += full_group_pieces(g, loop_planes, scalar_copy)
+                    pieces += full_group_pieces(g, scalar_copy)
             if block > 1 and half == 0:
                 find_max(block - 2)
             share = max(turn, (turn + 1) / 2)
@@ -728,16 +745,19 @@ def tile_differentialattention_pa_t_kernel(tc, x, Wq, Wk, lq1, lq2, lk1, lk2, ou
                         supers[before // 2][0],
                         (2 * half + i) * BANK_MATMULS,
                     )
-            for piece in pieces[:2]:
+            count = 4 if turn == total_turns - 1 else 2
+            for piece in pieces[:count]:
                 piece()
-            pieces = pieces[2:]
+            pieces = pieces[count:]
             if block > 1 and half == 0 and block % GROUP_BLOCKS == 1:
                 end = (block - 1) * BLOCK_T
-                pieces += finish_pieces(end - P, end, 0, (nc.gpsimd,), loop_bank)
+                pieces += finish_pieces(end)
             if turn == 2:
                 pieces += [find_lam_exps, find_neg_lam]
+        exponentiate_block(BLOCKS - 2)
         find_max(BLOCKS - 1)
         take_max_off(BLOCKS - 1, nc.vector)
-        last = finish_pieces(FULL_GROUPS * P, TENSOR_T, HALF, (nc.gpsimd, nc.vector), last_bank)
-        for piece in pieces + last:
+        exponentiate_block(BLOCKS - 1)
+        for piece in pieces:
             piece()
+        finish_last()

import math

import concourse.mybir as mybir
from concourse.masks import make_identity

F32 = mybir.dt.float32
BF16 = mybir.dt.bfloat16
I32 = mybir.dt.int32
U32 = mybir.dt.uint32
U8 = mybir.dt.uint8
FP8X4 = mybir.dt.float8_e4m3fn_x4
ALU = mybir.AluOpType
ACT = mybir.ActivationFunctionType
AXIS_X = mybir.AxisListType.X

P = 128
HALF = P // 2
QUADRANT = 32
TOKENS = 4 * 1024
C = 512
WORDS = C // 2
ROWS = 16
DIFFS = ROWS - 1
D = 64
HEADS = 8
BANK = 512
BANK_ROWS = 4
SCALE = D ** -0.5
LAM_INIT = 0.8 - 0.6 * math.exp(-0.3 * 12)

RUNS = 8
PAIRS = RUNS // 2
GROUP_TOKENS = P * RUNS
GROUPS = TOKENS // GROUP_TOKENS
FULL_GROUPS = 3
BLOCK_T = 32
GROUP_BLOCKS = P // BLOCK_T
SUPER_T = 2 * BLOCK_T
SUPER_COLS = SUPER_T * RUNS
HALF_T = 16
LAST_T = BLOCK_T + HALF_T
TENSOR_T = FULL_GROUPS * P + LAST_T
BLOCKS = FULL_GROUPS * GROUP_BLOCKS + 2
SUPERS = BLOCKS // 2
VECTOR_T = P - LAST_T
VECTOR_TILES = VECTOR_T * RUNS // P

VECTOR_COL = SUPERS * SUPER_COLS
X_COLS = VECTOR_COL + VECTOR_TILES * P
K_ROWS = BANK // (SUPER_T * PAIRS)

SCORE_COLS = DIFFS * PAIRS
BANK_MATMULS = 8

W_COLS = ROWS * D
PADDED = 2 * W_COLS + D
TILE_ROWS = BANK // D

VECTOR_ROWS = (2, 1)
STAGE_GAP = 3
SUM_LAG = 2

FLOPS = 2 * TOKENS * C * 2 * ROWS * D + 2 * TOKENS * ROWS * ROWS * D


def transpose_words(nc, planes, ident, rows_f32, blocks):
    for i, b in enumerate(blocks):
        for u in range(2):
            nc.tensor.transpose(
                planes[:, u, i * P : (i + 1) * P],
                rows_f32[:, b * WORDS + u : (b + 1) * WORDS : 2],
                ident[:],
            )


def tile_differentialattention_pa_t_kernel(tc, x, Wq, Wk, lq1, lq2, lk1, lk2, out):
    nc = tc.nc
    x_rows = x.flatten_outer_dims()
    out_rows = out.rearrange("b n a h -> (b n) (a h)")

    with (
        tc.tile_pool(name="keep", bufs=1) as keep,
        tc.tile_pool(name="stage", bufs=2) as stage,
        tc.tile_pool(name="tensor_way", bufs=1) as tensor_way,
        tc.tile_pool(name="vector_way", bufs=2) as vector_way,
        tc.tile_pool(name="products", bufs=6) as products,
        tc.psum_pool(name="psum_y", bufs=6) as psum_y,
        tc.psum_pool(name="psum_s", bufs=2) as psum_s,
        tc.manual_schedule(),
    ):
        ident = keep.tile([P, P], F32)
        make_identity(nc, ident[:])

        q_diag = []
        for turn in range(2):
            diag = keep.tile([P, BLOCK_T, PAIRS, 2, ROWS], F32, name="q_diag%d" % turn)
            nc.vector.memset(diag[:].rearrange("p t n s r -> p (t n s r)").bitcast(I32), 0)
            q_diag.append(diag)

        dense_flat = keep.tile([P, TENSOR_T * ROWS], F32, align_bytes=64)
        dense = dense_flat[:].rearrange("p (m t) -> p m t", t=TENSOR_T)
        w_words = {}
        for w in range(2):
            w_words[w] = dense_flat[:, w * 2 * W_COLS : (w + 1) * 2 * W_COLS]
        vec_words = dense_flat[:, 4 * W_COLS : 4 * W_COLS + 2 * VECTOR_TILES * P]
        last_first = 4 * W_COLS + 2 * VECTOR_TILES * P
        last_words = dense_flat[:, last_first : last_first + 2 * SUPER_COLS]

        nc.vector.memset(dense[:, DIFFS:], 0.0)

        w_codes = {}
        w_scales = {}
        w_padded = {}
        w_padded_scales = {}
        for w in (1, 0):
            w_codes[w] = keep.tile([P, W_COLS], U32, name="codes_%d" % w, align_bytes=64)
            w_scales[w] = keep.tile([P, W_COLS], U8, name="scales_%d" % w, align_bytes=64)
            w_padded[w] = keep.tile([P, PADDED], U32, name="padded_%d" % w, align_bytes=64)
            w_padded_scales[w] = keep.tile([P, PADDED], U8, name="padded_scales_%d" % w, align_bytes=64)
            for wide, words in ((w_padded[w], D), (w_padded_scales[w], D // 4)):
                gaps = wide[:].bitcast(I32)[:, : 2 * ROWS * words].rearrange(
                    "p (r z w) -> p r z w", z=2, w=words
                )
                nc.gpsimd.memset(gaps[:, :, 0, :], 0)
                nc.gpsimd.memset(wide[:].bitcast(I32)[:, 2 * ROWS * words :], 0)

        def copy_out(index, **operands):
            if index % 2 == 0:
                nc.scalar.copy(**operands)
            else:
                nc.vector.tensor_copy(**operands)

        w_loaded = {}
        x_words = {}

        def load_weight_part(w, W, part):
            w_sb = products.tile([P, HEADS // 2 * C], BF16, tag="prod")
            nc.sync.dma_start(
                out=w_sb[:].rearrange("p (a c) -> p a c", c=C),
                in_=W[part * 512 : (part + 1) * 512, :].rearrange("(a p) c -> p a c", p=P),
            )
            w_loaded[w, part] = w_sb[:].bitcast(F32)

        def load_group(g):
            x_sb = stage.tile([P, RUNS * C], BF16, tag="loaded", bufs=2)
            nc.sync.dma_start(
                out=x_sb[:],
                in_=x_rows[g * GROUP_TOKENS : (g + 1) * GROUP_TOKENS, :].rearrange(
                    "(t y) c -> t (y c)", y=RUNS
                ),
            )
            x_words[g] = x_sb[:].bitcast(F32)

        load_weight_part(1, Wk, 0)
        load_group(0)
        load_weight_part(1, Wk, 1)
        load_weight_part(0, Wq, 0)
        load_weight_part(0, Wq, 1)
        load_group(GROUPS - 1)
        vectors = keep.tile([P, 4, D], BF16)
        for v, vector in enumerate((lq1, lq2, lk1, lk2)):
            nc.sync.dma_start(out=vectors[:, v, :], in_=vector.partition_broadcast(P))

        def turn_weight_part(w, part):
            by_row = w_words[w].rearrange("p (a j d u) -> p a j d u", a=HEADS, j=2, d=D)
            for pair in range(2):
                a0 = part * HEADS // 2 + 2 * pair
                planes = psum_y.tile([P, 2, 2 * P], F32, name="planes", tag="y")
                transpose_words(nc, planes, ident, w_loaded[w, part], (2 * pair, 2 * pair + 1))
                by_j = planes[:].rearrange("p u (a d j) -> p j a d u", a=2, j=2)
                for j in range(2):
                    copy_out(pair, out=by_row[:, a0 : a0 + 2, j], in_=by_j[:, j])

        def quantise_weight_part(w, part):
            cols = slice(part * W_COLS // 2, (part + 1) * W_COLS // 2)
            nc.vector.quantize_mx(
                out=w_codes[w][:, cols].bitcast(FP8X4),
                scales=w_scales[w][:, cols],
                in_=w_words[w][:, part * W_COLS : (part + 1) * W_COLS].bitcast(BF16),
            )

        def pad_weight_part(w, part):
            rows = slice(part * ROWS // 2, (part + 1) * ROWS // 2)
            for narrow, wide, words in (
                (w_codes[w], w_padded[w], D),
                (w_scales[w], w_padded_scales[w], D // 4),
            ):
                nc.vector.tensor_copy(
                    out=wide[:].bitcast(I32)[:, words:].rearrange(
                        "p (r z w) -> p r z w", z=2, w=words
                    )[:, rows, 0, :],
                    in_=narrow[:].bitcast(I32).rearrange("p (r w) -> p r w", w=words)[:, rows],
                )

        x_codes = keep.tile([P, X_COLS], U32, align_bytes=64)
        x_scales = keep.tile([P, X_COLS], U8, align_bytes=64)

        def quantise_x(first, grouped):
            cols = slice(first, first + grouped.shape[1] // 4)
            nc.vector.quantize_mx(
                out=x_codes[:, cols].bitcast(FP8X4), scales=x_scales[:, cols], in_=grouped
            )

        def super_view(words):
            return words.rearrange(
                "p (b s t h n u) -> p b s h t n u", s=2, t=SUPER_T, h=2, n=2, u=2
            )

        def turn_runs(words, planes, s, h):
            first = 4 * h + s
            transpose_words(nc, planes, ident, words, (first, first + 2))

        def prepare_last_group():
            by_super = super_view(last_words)
            by_run = vec_words.rearrange("p (y t u) -> p y t u", y=RUNS, u=2)
            for h in range(2):
                for s in range(2):
                    planes = psum_y.tile([P, 2, 2 * P], F32, name="planes", tag="y")
                    turn_runs(x_words[GROUPS - 1], planes, s, h)
                    by_time = planes[:].rearrange("p u (n t) -> p n t u", n=2)
                    first = 4 * h + s
                    nc.scalar.copy(
                        out=by_run[:, first : first + 3 : 2], in_=by_time[:, :, LAST_T:, :]
                    )
                    nc.scalar.copy(
                        out=by_super[:, 0, s, h],
                        in_=planes[:].rearrange("p u (n t) -> p t n u", n=2)[:, :SUPER_T],
                    )

        def quantise_tiles(first, tiles):
            quantise_x(
                VECTOR_COL + first * P,
                vec_words[:, 2 * first * P : 2 * (first + tiles) * P].bitcast(BF16),
            )

        def full_group_pieces(g, copy):
            grouped = stage.tile([P, 4 * GROUP_TOKENS], BF16, tag="grouped", bufs=1, align_bytes=64)
            by_super = super_view(grouped[:].bitcast(F32))

            def turn(s, h):
                planes = psum_y.tile([P, 2, 2 * P], F32, name="planes", tag="y")
                turn_runs(x_words[g], planes, s, h)
                for b in range(2):
                    copy(
                        h,
                        out=by_super[:, b, s, h],
                        in_=planes[:].rearrange("p u (n b t) -> p b t n u", n=2, b=2)[:, b],
                    )

            def quantise(b):
                first = b * SUPER_COLS
                quantise_x(
                    g * GROUP_TOKENS + first, grouped[:, 4 * first : 4 * (first + SUPER_COLS)]
                )

            pieces = [lambda s=s, h=h: turn(s, h) for s in range(2) for h in range(2)]
            pieces += [lambda b=b: quantise(b) for b in range(2)]
            return pieces

        def scalar_copy(index, **operands):
            nc.scalar.copy(**operands)

        lam_products = keep.tile([P, 2, D], F32)
        lam_dots = keep.tile([P, 2], F32)
        lam_exps = keep.tile([P, 2], F32)
        neg_lam = keep.tile([P, 1], F32)

        def find_lam_dots():
            nc.vector.tensor_tensor(
                out=lam_products[:], in0=vectors[:, 0:2, :], in1=vectors[:, 2:4, :], op=ALU.mult
            )
            nc.vector.tensor_reduce(out=lam_dots[:], in_=lam_products[:], axis=AXIS_X, op=ALU.add)

        def find_lam_exps():
            nc.scalar.activation(out=lam_exps[:], in_=lam_dots[:], func=ACT.Exp)

        def find_neg_lam():
            nc.vector.tensor_tensor(
                out=neg_lam[:], in0=lam_exps[:, 1:2], in1=lam_exps[:, 0:1], op=ALU.subtract
            )
            nc.vector.tensor_scalar_add(out=neg_lam[:], in0=neg_lam[:], scalar1=-LAM_INIT)

        neg_max = keep.tile([P, TENSOR_T], F32)

        def project_pairs(bank, w, r, first, cols):
            for s in range(2):
                w_cols = slice(P * r + D * (1 - s), P * r + D * (1 - s) + P)
                x_cols = slice(first + s * SUPER_COLS // 2, first + s * SUPER_COLS // 2 + cols)
                nc.tensor.matmul_mx(
                    out=bank,
                    lhsT=w_padded[w][:, w_cols].bitcast(FP8X4),
                    lhsT_scale=w_padded_scales[w][:, w_cols],
                    rhs=x_codes[:, x_cols].bitcast(FP8X4),
                    rhs_scale=x_scales[:, x_cols],
                    start=(s == 0),
                    stop=(s == 1),
                )

        def block_times(block):
            return BLOCK_T if block < BLOCKS - 1 else HALF_T

        def open_super(index):
            k_pairs = tensor_way.tile([P, SUPER_T, DIFFS, PAIRS], F32, bufs=2)
            k_first = tensor_way.tile([P, SUPER_T, PAIRS], F32)
            return k_pairs, k_first

        def k_step(index, operands, bank_index):
            k_pairs, k_first = operands
            times = SUPER_T if index < SUPERS - 1 else LAST_T
            bank = psum_y.tile([P, K_ROWS, SUPER_T * PAIRS], F32, tag="y")
            for i in range(K_ROWS):
                r = bank_index * K_ROWS + i
                project_pairs(bank[:, i, :], 1, r, index * SUPER_COLS, SUPER_T * PAIRS)
            by_time = bank[:].rearrange("p i (t n) -> p t i n", n=PAIRS)[:, :times]
            skip = 1 if bank_index == 0 else 0
            if skip:
                nc.scalar.copy(out=k_first[:, :times], in_=by_time[:, :, 0])
            first = bank_index * K_ROWS + skip - 1
            count = K_ROWS - skip
            nc.vector.tensor_tensor(
                out=k_pairs[:, :times, first : first + count, :],
                in0=by_time[:, :, skip:],
                in1=k_first[:, :times].unsqueeze(2).to_broadcast([P, times, count, PAIRS]),
                op=ALU.subtract,
            )

        def q_step(block, diag, bank_index):
            cols = block_times(block) * PAIRS
            first = block // 2 * SUPER_COLS + block % 2 * BLOCK_T * PAIRS
            bank = psum_y.tile([P, BANK_ROWS, P], F32, tag="y")
            for i in range(BANK_ROWS):
                project_pairs(bank[:, i, :], 0, bank_index * BANK_ROWS + i, first, P)
            rows = slice(bank_index * BANK_ROWS, (bank_index + 1) * BANK_ROWS)
            by_token = diag[:].rearrange("p t n s r -> p s (t n) r")
            for s in range(2):
                half = slice(s * HALF, (s + 1) * HALF)
                nc.scalar.copy(
                    out=by_token[half, s, :cols, rows],
                    in_=bank[half, :, :cols].rearrange("p i c -> p c i"),
                )

        def score_step(block, diag, k_pairs, t0):
            raw = psum_s.tile([P, BANK_MATMULS, SCORE_COLS], F32, tag="raw")
            for i in range(BANK_MATMULS):
                nc.tensor.matmul(
                    out=raw[:, i, :],
                    lhsT=diag[:, t0 + i].rearrange("p n s r -> p (n s r)"),
                    rhs=k_pairs[:, block % 2 * BLOCK_T + t0 + i].rearrange("p m n -> p (m n)"),
                    start=True,
                    stop=True,
                )
            first = block * BLOCK_T + t0
            for n in range(PAIRS):
                quad = slice(n * QUADRANT, (n + 1) * QUADRANT)
                nc.scalar.copy(
                    out=dense[quad, :DIFFS, first : first + BANK_MATMULS],
                    in_=raw[quad].rearrange("p i (m n) -> p m i n", n=PAIRS)[:, :, :, n],
                )

        def find_max(block):
            first = block * BLOCK_T
            new = slice(first, first + block_times(block))
            nc.vector.tensor_reduce(
                out=neg_max[:, new],
                in_=dense[:, :, new].rearrange("p m t -> p t m"),
                axis=AXIS_X,
                op=ALU.max,
                negate=True,
            )

        def take_max_off(block, engine):
            first = block * BLOCK_T
            new = slice(first, first + block_times(block))
            shape = [P, ROWS, block_times(block)]
            engine.tensor_tensor(
                out=dense[:, :, new],
                in0=dense[:, :, new],
                in1=neg_max[:, new].unsqueeze(1).to_broadcast(shape),
                op=ALU.add,
            )

        def parts_of(factor):
            return factor[:].rearrange("p (e j) -> p j e", j=2)

        def store(first_new, end, result):
            nc.sync.dma_start(
                out=out_rows[first_new * RUNS : end * RUNS, :].rearrange(
                    "(t y) e -> t (y e)", y=RUNS
                ),
                in_=result[P - (end - first_new) :].rearrange("p e h -> p (e h)"),
            )

        def finish_pieces(end):
            first = end - P
            loaded = stage.tile([P, RUNS * C], BF16, tag="loaded", bufs=2)
            exps = loaded[:].bitcast(F32).rearrange("p (e m) -> p e m", m=ROWS)
            factor = tensor_way.tile([P, P], F32, bufs=2)
            by_j = parts_of(factor)

            def turn_and_exp(m0):
                flipped = psum_y.tile([P, BANK_ROWS, P], F32, tag="y")
                for i in range(BANK_ROWS):
                    nc.tensor.transpose(
                        flipped[:, i, :], dense[:, (m0 + i - 1) % ROWS, first:end], ident[:]
                    )
                nc.scalar.activation(
                    out=exps[:, :, m0 : m0 + BANK_ROWS],
                    in_=flipped[:].rearrange("p i e -> p e i"),
                    func=ACT.Exp,
                    scale=SCALE,
                )

            def find_factors():
                row_sum = tensor_way.tile([P, P], F32, bufs=2)
                nc.vector.tensor_reduce(out=row_sum[:], in_=exps, axis=AXIS_X, op=ALU.add)
                nc.vector.reciprocal(out=factor[:], in_=row_sum[:])

            def combine():
                nc.gpsimd.tensor_scalar(
                    out=by_j[:, 1], in0=by_j[:, 1], scalar1=neg_lam[:, 0:1], scalar2=None,
                    op0=ALU.mult,
                )
                by_parity = exps.rearrange("p (e j) (h i) -> p j i e h", j=2, i=2)
                shape = [P, RUNS * HEADS, HEADS]
                result = tensor_way.tile(shape, F32)
                odd_part = tensor_way.tile(shape, F32)
                for j, half in ((1, odd_part), (0, result)):
                    nc.gpsimd.tensor_tensor(
                        out=half[:],
                        in0=by_parity[:, j, j],
                        in1=by_j[:, j].unsqueeze(2).to_broadcast(shape),
                        op=ALU.mult,
                    )
                nc.gpsimd.tensor_tensor(
                    out=result[:], in0=result[:], in1=odd_part[:], op=ALU.add
                )
                store(first, end, result)

            pieces = [lambda m0=m0: turn_and_exp(m0) for m0 in range(0, ROWS, BANK_ROWS)]
            return pieces + [find_factors, lambda: None, combine]

        def exponentiate_block(block):
            first = block * BLOCK_T
            new = slice(first, first + block_times(block))
            nc.scalar.activation(
                out=dense[:, :, new], in_=dense[:, :, new], func=ACT.Exp, scale=SCALE
            )

        def finish_last():
            window = slice(TENSOR_T - P, TENSOR_T)
            lo = HALF
            sums = psum_y.tile([P, BANK_ROWS, P], F32, tag="y")
            for m in range(ROWS):
                nc.tensor.matmul(
                    out=sums[:, 0, :],
                    lhsT=dense[:, m, window],
                    rhs=ident[:],
                    start=(m == 0),
                    stop=(m == ROWS - 1),
                    is_transpose=True,
                )
            factor = tensor_way.tile([P, P], F32, bufs=2)
            by_j = parts_of(factor)
            nc.vector.reciprocal(out=factor[lo:], in_=sums[lo:, 0, :])
            nc.vector.tensor_scalar(
                out=by_j[lo:, 1], in0=by_j[lo:, 1], scalar1=neg_lam[lo:, 0:1], scalar2=None,
                op0=ALU.mult,
            )
            result = tensor_way.tile([P, RUNS * HEADS, HEADS], F32)
            odd_part = tensor_way.tile([P, RUNS * HEADS, HEADS], F32)
            for h0 in range(0, HEADS, BANK_ROWS):
                heads = slice(h0, h0 + BANK_ROWS)
                for j, half in ((1, odd_part), (0, result)):
                    flipped = psum_y.tile([P, BANK_ROWS, P], F32, tag="y")
                    for i in range(BANK_ROWS):
                        m = 2 * (h0 + i) + j
                        nc.tensor.transpose(
                            flipped[:, i, :], dense[:, (m - 1) % ROWS, window], ident[:]
                        )
                    nc.vector.tensor_tensor(
                        out=half[lo:, :, heads],
                        in0=flipped[lo:].rearrange("p i (e j) -> p j e i", j=2)[:, j],
                        in1=by_j[lo:, j].unsqueeze(2).to_broadcast(
                            [P - lo, RUNS * HEADS, BANK_ROWS]
                        ),
                        op=ALU.mult,
                    )
                nc.vector.tensor_tensor(
                    out=result[lo:, :, heads],
                    in0=result[lo:, :, heads],
                    in1=odd_part[lo:, :, heads],
                    op=ALU.add,
                )
            store(FULL_GROUPS * P, TENSOR_T, result)

        def project_tile(w, bank_index, tile_index):
            bank = psum_y.tile([P, BANK], F32, tag="y")
            tok = slice(VECTOR_COL + tile_index * P, VECTOR_COL + (tile_index + 1) * P)
            w_cols = slice(bank_index * BANK, (bank_index + 1) * BANK)
            nc.tensor.matmul_mx(
                out=bank[:],
                lhsT=x_codes[:, tok].bitcast(FP8X4),
                lhsT_scale=x_scales[:, tok],
                rhs=w_codes[w][:, w_cols].bitcast(FP8X4),
                rhs_scale=w_scales[w][:, w_cols],
                start=True,
                stop=True,
            )
            return bank[:].rearrange("p (i d) -> p i d", d=D)

        def open_tile(tile_index):
            q_sb = vector_way.tile([P, ROWS, D], F32)
            k_sb = vector_way.tile([P, DIFFS, D], F32)
            return q_sb, k_sb

        def fill_k(tile_index, operands):
            q_sb, k_sb = operands
            k_zero = vector_way.tile([P, D], F32)
            for bank_index in range(ROWS // TILE_ROWS):
                bank = project_tile(1, bank_index, tile_index)
                skip = 1 if bank_index == 0 else 0
                if skip:
                    nc.scalar.copy(out=k_zero[:], in_=bank[:, 0])
                first = bank_index * TILE_ROWS + skip - 1
                count = TILE_ROWS - skip
                nc.vector.tensor_tensor(
                    out=k_sb[:, first : first + count, :],
                    in0=bank[:, skip:],
                    in1=k_zero[:].unsqueeze(1).to_broadcast([P, count, D]),
                    op=ALU.subtract,
                )

        def fill_q(tile_index, operands):
            q_sb, k_sb = operands
            made = []
            for bank_index in range(ROWS // TILE_ROWS):
                bank = project_tile(0, bank_index, tile_index)
                skip = VECTOR_ROWS[bank_index]
                nc.scalar.copy(
                    out=q_sb[:, bank_index * TILE_ROWS + skip : (bank_index + 1) * TILE_ROWS, :],
                    in_=bank[:, skip:],
                )
                for r in range(skip):
                    prod = multiply_row(nc.vector, bank[:, r, :], k_sb)
                    made.append((prod, tile_index, bank_index * TILE_ROWS + r))
            return made

        def multiply_row(engine, q_row, k_sb):
            prod = products.tile([P, DIFFS, D], F32, tag="prod")
            engine.tensor_tensor(
                out=prod[:],
                in0=q_row.unsqueeze(1).to_broadcast([P, DIFFS, D]),
                in1=k_sb[:],
                op=ALU.mult,
            )
            return prod

        def batch_stages(first_tile, tiles, batch):
            batch_rows = tiles * ROWS
            batch_shape = [P, batch_rows, ROWS]
            row_max = vector_way.tile([P, batch_rows], F32)
            row_sum = vector_way.tile([P, batch_rows], F32)
            factor = vector_way.tile([P, batch_rows], F32)
            odd_rows = factor[:].rearrange("p (e j) -> p e j", j=2)[:, :, 1]

            def find_row_max():
                nc.vector.tensor_reduce(out=row_max[:], in_=batch[:], axis=AXIS_X, op=ALU.max)

            def take_off():
                nc.gpsimd.tensor_tensor(
                    out=batch[:],
                    in0=batch[:],
                    in1=row_max[:].unsqueeze(2).to_broadcast(batch_shape),
                    op=ALU.subtract,
                )

            def exponentiate():
                nc.scalar.activation(out=batch[:], in_=batch[:], func=ACT.Exp, scale=SCALE)

            def find_row_factors():
                nc.vector.tensor_reduce(out=row_sum[:], in_=batch[:], axis=AXIS_X, op=ALU.add)
                nc.vector.reciprocal(out=factor[:], in_=row_sum[:])

            def scale_rows():
                nc.gpsimd.tensor_scalar(
                    out=odd_rows, in0=odd_rows, scalar1=neg_lam[:, 0:1], scalar2=None, op0=ALU.mult
                )
                nc.gpsimd.tensor_tensor(
                    out=batch[:],
                    in0=batch[:],
                    in1=factor[:].unsqueeze(2).to_broadcast(batch_shape),
                    op=ALU.mult,
                )

            def store():
                by_parity = batch[:].rearrange("p (e j) (h i) -> p e j h i", j=2, i=2)
                result = vector_way.tile([P, tiles * HEADS, HEADS], F32)
                nc.gpsimd.tensor_tensor(
                    out=result[:],
                    in0=by_parity[:, :, 0, :, 0],
                    in1=by_parity[:, :, 1, :, 1],
                    op=ALU.add,
                )
                by_run = out_rows.rearrange("(t y) e -> y t e", y=RUNS)
                for v in range(tiles):
                    at = (first_tile + v) * P
                    stop = at + P
                    p0 = 0
                    while at < stop:
                        y, t = divmod(at, VECTOR_T)
                        count = min(VECTOR_T - t, stop - at)
                        nc.sync.dma_start(
                            out=by_run[y, TENSOR_T + t : TENSOR_T + t + count, :],
                            in_=result[p0 : p0 + count, v * HEADS : (v + 1) * HEADS, :].rearrange(
                                "p a h -> p (a h)"
                            ),
                        )
                        at += count
                        p0 += count

            def pause():
                pass

            return [find_row_max, take_off, pause, exponentiate, find_row_factors, scale_rows, store]

        BATCHES = ((0, 3), (3, 2))
        tiles_open = {}
        scores_of = {}
        waiting = []
        stages = []

        def sum_oldest():
            prod, tile_index, r = waiting.pop(0)
            nc.vector.tensor_reduce(
                out=scores_of[tile_index][:, r, 1:], in_=prod[:], axis=AXIS_X, op=ALU.add
            )
            if r == ROWS - 1:
                for first_tile, tiles in BATCHES:
                    if tile_index == first_tile + tiles - 1:
                        stages.extend(batch_stages(first_tile, tiles, scores_of["batch", first_tile]))

        def next_stage(unit):
            if stages and unit % STAGE_GAP == 0:
                stages.pop(0)()

        def open_k(tile_index):
            tiles_open[tile_index] = open_tile(tile_index)
            for first_tile, tiles in BATCHES:
                if tile_index == first_tile:
                    batch = vector_way.tile([P, tiles * ROWS, ROWS], F32)
                    nc.vector.memset(batch[:, :, 0:1], 0.0)
                    scores_of["batch", first_tile] = batch
                    for v in range(tiles):
                        scores_of[first_tile + v] = batch[:, v * ROWS : (v + 1) * ROWS, :]
            fill_k(tile_index, tiles_open[tile_index])

        def open_q(tile_index):
            waiting.extend(fill_q(tile_index, tiles_open[tile_index]))

        def row_unit(tile_index, r):
            next_stage(r)
            q_sb, k_sb = tiles_open[tile_index]
            waiting.append((multiply_row(nc.gpsimd, q_sb[:, r, :], k_sb), tile_index, r))
            if tile_index + 1 < VECTOR_TILES and r == ROWS - 5:
                open_k(tile_index + 1)
            if tile_index + 1 < VECTOR_TILES and r == ROWS - 4:
                open_q(tile_index + 1)
            while len(waiting) > SUM_LAG:
                sum_oldest()

        units = [
            lambda v=v, r=r: row_unit(v, r)
            for v in range(VECTOR_TILES)
            for r in range(ROWS)
            if r % TILE_ROWS >= VECTOR_ROWS[r // TILE_ROWS]
        ]
        units += [sum_oldest] * SUM_LAG + [lambda: next_stage(0)] * 7

        LEAD = 2
        total_turns = 2 * BLOCKS
        supers = {}

        def k_turn(turn):
            index, quarter = divmod(turn, 4)
            if index < SUPERS:
                if quarter == 0:
                    supers[index] = open_super(index)
                for i in range(2):
                    k_step(index, supers[index], 2 * quarter + i)

        turn_weight_part(1, 0)
        quantise_weight_part(1, 0)
        first_group = full_group_pieces(0, copy_out)
        for piece in first_group[:4]:
            piece()
        load_group(1)
        pad_weight_part(1, 0)
        first_group[4]()
        turn_weight_part(1, 1)
        k_turn(0)
        quantise_weight_part(1, 1)
        pad_weight_part(1, 1)
        turn_weight_part(0, 0)
        quantise_weight_part(0, 0)
        k_turn(1)
        turn_weight_part(0, 1)
        quantise_weight_part(0, 1)
        prepare_last_group()
        load_group(2)
        quantise_tiles(0, 2)
        pad_weight_part(0, 0)
        pad_weight_part(0, 1)
        open_k(0)
        open_q(0)
        first_group[5]()
        quantise_tiles(2, 2)
        quantise_tiles(4, 1)
        quantise_x(FULL_GROUPS * GROUP_TOKENS, last_words.bitcast(BF16))
        find_lam_dots()
        pieces = []
        done = 0
        for turn in range(total_turns + 1):
            block, half = divmod(turn, 2)
            k_turn(turn + LEAD)
            if block < BLOCKS:
                for i in range(2):
                    q_step(block, q_diag[block % 2], 2 * half + i)
                g = block // GROUP_BLOCKS + 1
                if half == 0 and block % GROUP_BLOCKS == 0 and g < FULL_GROUPS:
                    pieces += full_group_pieces(g, scalar_copy)
            if block > 1 and half == 0:
                find_max(block - 2)
            share = max(turn, (turn + 1) / 2)
            while done < len(units) and done * (total_turns - 1) < share * len(units):
                units[done]()
                done += 1
            if block > 1 and half == 0:
                take_max_off(block - 2, nc.gpsimd)
            before = block - 1
            if block > 0:
                for i in range(2):
                    score_step(
                        before,
                        q_diag[before % 2],
                        supers[before // 2][0],
                        (2 * half + i) * BANK_MATMULS,
                    )
            count = 4 if turn == total_turns - 1 else 2
            for piece in pieces[:count]:
                piece()
            pieces = pieces[count:]
            if block > 1 and half == 0 and block % GROUP_BLOCKS == 1:
                end = (block - 1) * BLOCK_T
                pieces += finish_pieces(end)
            if turn == 2:
                pieces += [find_lam_exps, find_neg_lam]
        exponentiate_block(BLOCKS - 2)
        find_max(BLOCKS - 1)
        take_max_off(BLOCKS - 1, nc.vector)
        exponentiate_block(BLOCKS - 1)
        for piece in pieces:
            piece()
        finish_last()
